import numpy as np
import ml_dtypes


BF16 = ml_dtypes.bfloat16


def bf(x):
    return np.asarray(x, np.float32).astype(BF16)


def f64(x):
    return np.asarray(x).astype(np.float64)


E2M1 = np.array([0.0, 0.5, 1.0, 1.5, 2.0, 3.0, 4.0, 6.0, -0.0, -0.5, -1.0, -1.5, -2.0, -3.0, -4.0, -6.0])


def pack_weight(w, fmt):
    k, n = w.shape
    w = f64(bf(w)).reshape(k // 32, 32, n)
    amax = np.abs(w).max(1)
    if fmt == "e4m3":
        byte = np.frexp(amax)[1] - 1 + 127 - 7
    else:
        mant, ex = np.frexp(amax / 6.0)
        byte = np.where(mant > 0.5, ex, ex - 1) + 127
    byte = np.clip(np.where(amax > 0, byte, 1), 1, 254)
    scaled = (w * np.exp2(127.0 - byte)[:, None, :]).reshape(k, n).astype(np.float32)
    by_word = np.ascontiguousarray(scaled.reshape(k // 512, 128, 4, n).transpose(0, 1, 3, 2))
    if fmt == "e4m3":
        words = by_word.astype(ml_dtypes.float8_e4m3fn).view(np.uint8)
    else:
        c = by_word.astype(ml_dtypes.float4_e2m1fn).view(np.uint8) & 0xF
        words = c[..., 0::2] | (c[..., 1::2] << 4)
    return np.ascontiguousarray(words), np.ascontiguousarray(byte.astype(np.uint8).reshape(k // 512, 16, n))


def unpack_weight(words, scales, fmt):
    g, p, n, _ = words.shape
    if fmt == "e4m3":
        vals = np.ascontiguousarray(words).view(ml_dtypes.float8_e4m3fn).astype(np.float64)
    else:
        nib = np.empty((g, p, n, 4), np.uint8)
        nib[..., 0::2] = words & 0xF
        nib[..., 1::2] = words >> 4
        vals = E2M1[nib]
    vals = vals * np.repeat(np.exp2(scales.astype(np.float64) - 127.0), 8, axis=1)[..., None]
    return vals.transpose(0, 1, 3, 2).reshape(g * 512, n)

def pack4(w):
    words, scales = pack_weight(w, "e2m1")
    return words.reshape(words.shape[0], 128, -1), scales


def unpack4(words, scales):
    return unpack_weight(words.reshape(words.shape[0], 128, -1, 2), scales, "e2m1")


def kspread(k):
    return np.exp2(np.repeat(np.random.randint(-6, 7, k // 32), 32).astype(np.float64))


B, V, H = 384, 128, 4096
G = 4 * H
EPS = 1e-5


def sigmoid(v):
    return 1.0 / (1.0 + np.exp(-v))


def layer_norm(v, w, b):
    mu = v.mean(-1, keepdims=True)
    var = ((v - mu) ** 2).mean(-1, keepdims=True)
    return (v - mu) / np.sqrt(var + EPS) * w + b


def setup_inputs():
    s = kspread(H)
    x = bf(np.random.standard_normal((B, V)))
    h0 = np.random.standard_normal((B, H)) * s
    h0_words, h0_scales = pack4(np.ascontiguousarray(h0.T))
    c0 = bf(np.random.standard_normal((B, H)))
    w_ih1 = bf(np.random.standard_normal((G, V)) / np.sqrt(V))
    w_hh1 = np.random.standard_normal((G, H)) / np.sqrt(H) / s
    w_hh1_words, w_hh1_scales = pack4(np.ascontiguousarray(w_hh1.T))
    return {"x": x,
            "h0_words": h0_words,
            "h0_scales": h0_scales,
            "c0": c0,
            "w_ih1": w_ih1,
            "w_hh1_words": w_hh1_words,
            "w_hh1_scales": w_hh1_scales,
            "lni_w1": bf(1.0 + 0.1 * np.random.standard_normal(G)),
            "lni_b1": bf(0.1 * np.random.standard_normal(G)),
            "lnh_w1": bf(1.0 + 0.1 * np.random.standard_normal(G)),
            "lnh_b1": bf(0.1 * np.random.standard_normal(G)),
            "lnc_w1": bf(1.0 + 0.1 * np.random.standard_normal(H)),
            "lnc_b1": bf(0.1 * np.random.standard_normal(H))}


def reference(x, h0_words, h0_scales, c0, w_ih1, w_hh1_words, w_hh1_scales, lni_w1, lni_b1, lnh_w1, lnh_b1, lnc_w1, lnc_b1):
    a = f64(x) @ f64(w_ih1).T
    r = unpack4(h0_words, h0_scales).T @ unpack4(w_hh1_words, w_hh1_scales)
    gates = layer_norm(a, f64(lni_w1), f64(lni_b1)) + layer_norm(r, f64(lnh_w1), f64(lnh_b1))
    i, f, g, o = np.split(gates, 4, axis=1)
    cy = layer_norm(sigmoid(f) * f64(c0) + sigmoid(i) * np.tanh(g), f64(lnc_w1), f64(lnc_b1))
    hy = sigmoid(o) * np.tanh(cy)
    return hy, cy

@@ -1,0 +1,306 @@
+from contextlib import ExitStack
+
+import concourse.mybir as mybir
+from concourse.masks import make_identity
+
+F32 = mybir.dt.float32
+BF16 = mybir.dt.bfloat16
+U8 = mybir.dt.uint8
+I32 = mybir.dt.int32
+FP4X4 = mybir.dt.float4_e2m1fn_x4
+ALU = mybir.AluOpType
+ACT = mybir.ActivationFunctionType
+
+B, V, H = 384, 128, 4096
+G = 4 * H
+EPS = 1e-5
+FLOPS = 2 * B * (H + V) * G
+
+P = 128
+NT = B // P
+NBLK = 512
+NB = G // NBLK
+NJ = H // NBLK
+KP = H // 512
+NBUF = 3
+NWN = 3
+NBIG = 5
+WPAD = 144
+GN = 132
+
+
+def tile_multilstm_pa_kernel(
+    tc, x, h0_words, h0_scales, c0, w_ih1, w_hh1_words, w_hh1_scales,
+    lni_w1, lni_b1, lnh_w1, lnh_b1, lnc_w1, lnc_b1, out_0, out_1,
+):
+    nc = tc.nc
+
+    def out_block(dst, t, j):
+        return dst[P * t : P * (t + 1), NBLK * j : NBLK * (j + 1)]
+
+    with ExitStack() as ctx:
+        keep = ctx.enter_context(tc.tile_pool(name="keep", bufs=1))
+        psum = ctx.enter_context(tc.psum_pool(name="psum", bufs=1))
+
+        warm = keep.tile([P, 1], F32, name="warm")
+        nc.vector.memset(warm[:], 0.0)
+        nc.scalar.activation(out=warm[:], in_=warm[:], func=ACT.Sigmoid)
+
+        ident_f = keep.tile([P, P], F32, name="ident_f")
+        make_identity(nc, ident_f[:])
+        ident_b = keep.tile([P, P], BF16, name="ident_b")
+        make_identity(nc, ident_b[:])
+
+        wi_col = keep.tile([P, P], F32, name="wi_col")
+        w3t = keep.tile([P, NB, NBLK], F32, name="w3t")
+        fo = keep.tile([P, NT, 2, NJ, NBLK], F32, name="fo")
+        bnr = keep.tile([P, NT, NB, 6], F32, name="bnr")
+        bnc = keep.tile([P, NT, NJ, 6], F32, name="bnc")
+        x_f = keep.tile([P, NT, V], F32, name="x_f")
+        xst = keep.tile([P, NT, V], F32, name="xst")
+        cmat = keep.tile([P, NT, P], BF16, name="cmat")
+        coeft = keep.tile([P, NT, P], BF16, name="coeft")
+        mhalf = keep.tile([P, NT, 1], F32, name="mhalf")
+        mvr = keep.tile([P, NT, 2], F32, name="mvr")
+        mvc = keep.tile([P, NT, 2], F32, name="mvc")
+        ve_r = keep.tile([P, NT, 1], F32, name="ve_r")
+        ve_c = keep.tile([P, NT, 1], F32, name="ve_c")
+        rstd_r = keep.tile([P, NT, 1], F32, name="rstd_r")
+        rstd_c = keep.tile([P, NT, 1], F32, name="rstd_c")
+        negc = keep.tile([P, NT, 1], F32, name="negc")
+        rem_r = keep.tile([P, NT, 2], F32, name="rem_r")
+
+        def split3(src, rem, cm, col):
+            nc.vector.tensor_copy(out=cm[:, :, col : col + 1], in_=src)
+            nc.vector.tensor_tensor(out=rem[:, :, 0:1], in0=src, in1=cm[:, :, col : col + 1], op=ALU.subtract)
+            nc.vector.tensor_copy(out=cm[:, :, col + 1 : col + 2], in_=rem[:, :, 0:1])
+            nc.vector.tensor_tensor(out=rem[:, :, 1:2], in0=rem[:, :, 0:1], in1=cm[:, :, col + 1 : col + 2], op=ALU.subtract)
+            nc.vector.tensor_copy(out=cm[:, :, col + 2 : col + 3], in_=rem[:, :, 1:2])
+
+        with tc.tile_pool(name="stream", bufs=1) as one:
+            h0c = one.tile([P, KP, 2 * B], U8, name="h0c", align_bytes=64)
+            h0s = one.tile([P, KP, B], U8, name="h0s", align_bytes=64)
+            wcod = [one.tile([P, KP, 2 * NBLK], U8, name="wcod%d" % i, align_bytes=64) for i in range(NBUF)]
+            wpl = [one.tile([P, KP, NBLK], U8, name="wpl%d" % i, align_bytes=64) for i in range(NBUF)]
+            wnat = [one.tile([P, 4, WPAD], BF16, name="wnat%d" % i) for i in range(NWN)]
+
+            nc.sync.dma_start(out=h0c[:], in_=h0_words.rearrange("g p n -> p g n"))
+            nc.vector.memset(h0s[:].bitcast(I32), 0)
+            for i in range(NBUF):
+                nc.vector.memset(wpl[i][:].bitcast(I32), 0)
+            for q4 in range(4):
+                nc.sync.dma_start(
+                    out=h0s[32 * q4 : 32 * q4 + 4, :, :].bitcast(I32),
+                    in_=h0_scales[:, 4 * q4 : 4 * q4 + 4, :].rearrange("g r n -> r g n").bitcast(I32),
+                )
+            for i in range(NWN):
+                nc.vector.memset(wnat[i][:], 1.0)
+            nc.vector.memset(cmat[:], 0.0)
+            nc.vector.memset(cmat[:, :, 0:2], 1.0)
+            nc.vector.memset(mhalf[:], -0.5)
+
+            x_bf = one.tile([P, NT, V], BF16, name="x_bf")
+            nc.scalar.dma_start(out=x_bf[:], in_=x.rearrange("(t p) k -> p t k", p=P))
+            nc.vector.tensor_copy(out=x_f[:], in_=x_bf[:])
+            wi_nat = one.tile([P, P], BF16, name="wi_nat")
+            nc.scalar.dma_start(out=wi_nat[:], in_=lni_w1.rearrange("(c p) -> c p", p=P))
+            wi_ps = psum.tile([P, P], BF16, tag="misc", bufs=2, name="wi_ps")
+            nc.tensor.transpose(wi_ps[:], wi_nat[:], ident_b[:])
+            nc.vector.tensor_copy(out=wi_col[:], in_=wi_ps[:])
+
+            xt_ps = psum.tile([P, NT, V], F32, tag="misc", bufs=2, name="xt_ps")
+            for t in range(NT):
+                nc.tensor.transpose(xt_ps[:, t, :], x_f[:, t, :], ident_f[:])
+            xt_f = one.tile([P, NT, V], F32, name="xt_f")
+            nc.vector.tensor_copy(out=xt_f[:], in_=xt_ps[:])
+
+            gram = psum.tile([P, GN], F32, tag="gram", bufs=1, name="gram")
+
+            def make_w3(b):
+                wn = wnat[b % NWN]
+                nc.scalar.dma_start(
+                    out=wn[:, :, 0:V],
+                    in_=w_ih1[NBLK * b : NBLK * (b + 1), :].rearrange("(s p) k -> p s k", p=P),
+                )
+                w3n = one.tile([P, 4, V], F32, tag="w3n", bufs=2, name="w3n")
+                for s in range(4):
+                    nc.tensor.matmul(
+                        out=gram[:], lhsT=wn[:, s, 0:V], rhs=wn[:, s, 0:GN],
+                        start=(b == 0 and s == 0), stop=(b == NB - 1 and s == 3),
+                    )
+                    nc.scalar.activation(
+                        out=w3n[:, s, :], in_=wn[:, s, 0:V], func=ACT.Copy,
+                        scale=wi_col[:, 4 * b + s : 4 * b + s + 1],
+                    )
+                tp = psum.tile([P, NBLK], F32, tag="big", bufs=NBIG, name="tp")
+                for s in range(4):
+                    nc.tensor.transpose(tp[:, V * s : V * (s + 1)], w3n[:, s, :], ident_f[:])
+                nc.scalar.copy(out=w3t[:, b, :], in_=tp[:])
+
+            def a_stats():
+                gs = one.tile([P, GN], F32, name="gs")
+                nc.vector.tensor_copy(out=gs[:], in_=gram[:])
+                y = psum.tile([P, NT, GN], F32, tag="misc", bufs=2, name="y")
+                for t in range(NT):
+                    nc.tensor.matmul(out=y[:, t, :], lhsT=xt_f[:, t, :], rhs=gs[:], start=True, stop=True)
+                ssq = one.tile([P, NT, 1], F32, name="ssq")
+                prod = one.tile([P, V], F32, name="prod")
+                for t in range(NT):
+                    nc.vector.scalar_tensor_tensor(
+                        out=prod[:], in0=y[:, t, 0:V], scalar=1.0, in1=x_f[:, t, :],
+                        op0=ALU.mult, op1=ALU.mult, accum_out=ssq[:, t, :],
+                    )
+                mean_a = one.tile([P, NT, 1], F32, name="mean_a")
+                nc.vector.tensor_single_scalar(out=mean_a[:], in_=y[:, :, V : V + 1], scalar=1.0 / G, op=ALU.mult)
+                msq = one.tile([P, NT, 1], F32, name="msq")
+                nc.vector.tensor_tensor(out=msq[:], in0=mean_a[:], in1=mean_a[:], op=ALU.mult)
+                var_a = one.tile([P, NT, 1], F32, name="var_a")
+                nc.vector.scalar_tensor_tensor(
+                    out=var_a[:], in0=ssq[:], scalar=1.0 / G, in1=msq[:], op0=ALU.mult, op1=ALU.subtract,
+                )
+                nc.gpsimd.tensor_single_scalar(out=var_a[:], in_=var_a[:], scalar=EPS, op=ALU.add)
+                rstd_a = one.tile([P, NT, 1], F32, name="rstd_a")
+                nc.gpsimd.tensor_tensor(out=rstd_a[:], in0=var_a[:], in1=mhalf[:], op=ALU.pow)
+                negma = one.tile([P, NT, 1], F32, name="negma")
+                nc.vector.scalar_tensor_tensor(
+                    out=negma[:], in0=mean_a[:], scalar=-1.0, in1=rstd_a[:], op0=ALU.mult, op1=ALU.mult,
+                )
+                rem_a = one.tile([P, NT, 2], F32, name="rem_a")
+                split3(negma[:], rem_a, cmat, 5)
+                xs = one.tile([P, NT, V], F32, name="xs")
+                xs_ps = psum.tile([P, NT, V], F32, tag="misc", bufs=2, name="xs_ps")
+                for t in range(NT):
+                    nc.vector.tensor_scalar_mul(out=xs[:, t, :], in0=x_f[:, t, :], scalar1=rstd_a[:, t, :])
+                    nc.tensor.transpose(xs_ps[:, t, :], xs[:, t, :], ident_f[:])
+                nc.vector.tensor_copy(out=xst[:], in_=xs_ps[:])
+
+            for b in range(NB):
+                cod, pl = wcod[b % NBUF], wpl[b % NBUF]
+                for q4 in range(4):
+                    nc.sync.dma_start(
+                        out=pl[32 * q4 : 32 * q4 + 4, :, :].bitcast(I32),
+                        in_=w_hh1_scales[:, 4 * q4 : 4 * q4 + 4, NBLK * b : NBLK * (b + 1)]
+                        .rearrange("g r n -> r g n").bitcast(I32),
+                    )
+                nc.sync.dma_start(
+                    out=cod[:],
+                    in_=w_hh1_words[:, :, 2 * NBLK * b : 2 * NBLK * (b + 1)].rearrange("g p n -> p g n"),
+                )
+                whb = one.tile([P, NBLK], BF16, tag="whb", bufs=3, name="whb")
+                nc.sync.dma_start(out=whb[:], in_=lnh_w1[NBLK * b : NBLK * (b + 1)].partition_broadcast(P))
+
+                q, j = b // NJ, b % NJ
+                for t in range(NT):
+                    acc = psum.tile([P, NBLK], F32, tag="big", bufs=NBIG, name="acc")
+                    for g in range(KP):
+                        nc.tensor.matmul_mx(
+                            out=acc[:],
+                            lhsT=h0c[:, g, 2 * P * t : 2 * P * (t + 1)].bitcast(FP4X4),
+                            lhsT_scale=h0s[:, g, P * t : P * (t + 1)],
+                            rhs=cod[:, g, :].bitcast(FP4X4),
+                            rhs_scale=pl[:, g, :],
+                            start=(g == 0),
+                            stop=(g == KP - 1),
+                        )
+                    nc.vector.bn_stats(out=bnr[:, t, b, :], in_=acc[:])
+                    if q % 2 == 1:
+                        nc.vector.tensor_tensor(out=fo[:, t, q // 2, j, :], in0=acc[:], in1=whb[:], op=ALU.mult)
+                    else:
+                        stg = one.tile([P, NBLK], F32, tag="stg", bufs=3, name="stg")
+                        nc.vector.tensor_tensor(out=stg[:], in0=acc[:], in1=whb[:], op=ALU.mult)
+                        nc.gpsimd.dma_start(out=out_block(out_0 if q == 0 else out_1, t, j), in_=stg[:])
+                if b < NB // 2:
+                    make_w3(2 * b)
+                    make_w3(2 * b + 1)
+                if b == NB // 2:
+                    a_stats()
+
+        with tc.tile_pool(name="tail", bufs=1) as tail:
+            rows = [tail.tile([P, 4, NBLK], BF16, name="rows%d" % i) for i in range(2)]
+            for i in range(2):
+                nc.gpsimd.memset(rows[i][:], 0.0)
+            wc = tail.tile([P, H], BF16, name="wc")
+            bc = tail.tile([P, H], BF16, name="bc")
+
+            def coef(t):
+                nc.vector.bn_aggr(out=mvr[:, t, :], in_=bnr[:, t, :, :].rearrange("p b s -> p (b s)"))
+                nc.gpsimd.tensor_single_scalar(out=ve_r[:, t, :], in_=mvr[:, t, 1:2], scalar=EPS, op=ALU.add)
+                nc.gpsimd.tensor_tensor(out=rstd_r[:, t, :], in0=ve_r[:, t, :], in1=mhalf[:, t, :], op=ALU.pow)
+                nc.vector.scalar_tensor_tensor(
+                    out=negc[:, t, :], in0=mvr[:, t, 0:1], scalar=-1.0, in1=rstd_r[:, t, :],
+                    op0=ALU.mult, op1=ALU.mult,
+                )
+                split3(negc[:, t : t + 1, :], rem_r[:, t : t + 1, :], cmat[:, t : t + 1, :], 2)
+                pc = psum.tile([P, P], BF16, tag="misc", bufs=2, name="pc")
+                nc.tensor.transpose(pc[:], cmat[:, t, :], ident_b[:])
+                nc.vector.tensor_copy(out=coeft[:, t, :], in_=pc[:])
+
+            live = {}
+
+            def vec_rows(vec, j, n):
+                return vec.rearrange("(q j n) -> q j n", q=4, j=NJ)[:, j, :].partition_broadcast(n)
+
+            def gates(t, j):
+                rw = rows[(t * NJ + j) % 2]
+                nc.sync.dma_start(out=rw[0:1, :, :], in_=vec_rows(lni_b1, j, 1))
+                nc.sync.dma_start(out=rw[1:2, :, :], in_=vec_rows(lnh_b1, j, 1))
+                nc.sync.dma_start(out=rw[2:5, :, :], in_=vec_rows(lnh_w1, j, 3))
+                nc.sync.dma_start(out=rw[5:8, :, :], in_=vec_rows(lni_w1, j, 3))
+                ri = tail.tile([P, NBLK], F32, tag="rb", bufs=8, name="ri")
+                nc.sync.dma_start(out=ri[:], in_=out_block(out_0, t, j))
+                rg = tail.tile([P, NBLK], F32, tag="rb", bufs=8, name="rg")
+                nc.sync.dma_start(out=rg[:], in_=out_block(out_1, t, j))
+                c0b = tail.tile([P, NBLK], BF16, tag="c0b", bufs=3, name="c0b")
+                nc.sync.dma_start(out=c0b[:], in_=out_block(c0, t, j))
+                live[(t, j)] = (ri, rg, c0b)
+                for q, chunk in ((0, ri[:]), (2, rg[:]), (1, fo[:, t, 0, j, :]), (3, fo[:, t, 1, j, :])):
+                    pg = psum.tile([P, NBLK], F32, tag="big", bufs=NBIG, name="pg")
+                    nc.tensor.matmul(out=pg[:], lhsT=xst[:, t, :], rhs=w3t[:, NJ * q + j, :], start=True, stop=False)
+                    nc.tensor.matmul(out=pg[:], lhsT=coeft[:, t, :], rhs=rw[:, q, :], start=False, stop=True)
+                    nc.vector.scalar_tensor_tensor(
+                        out=chunk, in0=chunk, scalar=rstd_r[:, t, :], in1=pg[:], op0=ALU.mult, op1=ALU.add,
+                    )
+                    nc.scalar.activation(out=chunk, in_=chunk, func=(ACT.Tanh if q == 2 else ACT.Sigmoid))
+
+            def combine(t, j):
+                ri, rg, c0b = live[(t, j)]
+                f = fo[:, t, 0, j, :]
+                nc.vector.tensor_tensor(out=ri[:], in0=ri[:], in1=rg[:], op=ALU.mult)
+                nc.vector.tensor_tensor(out=f, in0=f, in1=c0b[:], op=ALU.mult)
+                nc.vector.tensor_tensor(out=f, in0=f, in1=ri[:], op=ALU.add)
+                nc.vector.bn_stats(out=bnc[:, t, j, :], in_=f)
+
+            def c_stats(t):
+                nc.vector.bn_aggr(out=mvc[:, t, :], in_=bnc[:, t, :, :].rearrange("p b s -> p (b s)"))
+                nc.gpsimd.tensor_single_scalar(out=ve_c[:, t, :], in_=mvc[:, t, 1:2], scalar=EPS, op=ALU.add)
+                nc.gpsimd.tensor_tensor(out=rstd_c[:, t, :], in0=ve_c[:, t, :], in1=mhalf[:, t, :], op=ALU.pow)
+
+            def finish(t, j):
+                f, o = fo[:, t, 0, j, :], fo[:, t, 1, j, :]
+                cols = slice(NBLK * j, NBLK * (j + 1))
+                nc.vector.scalar_tensor_tensor(
+                    out=f, in0=f, scalar=mvc[:, t, 0:1], in1=wc[:, cols], op0=ALU.subtract, op1=ALU.mult,
+                )
+                nc.vector.scalar_tensor_tensor(
+                    out=f, in0=f, scalar=rstd_c[:, t, :], in1=bc[:, cols], op0=ALU.mult, op1=ALU.add,
+                )
+                th = tail.tile([P, NBLK], F32, tag="th", bufs=2, name="th")
+                nc.scalar.activation(out=th[:], in_=f, func=ACT.Tanh)
+                nc.scalar.dma_start(out=out_block(out_1, t, j), in_=f)
+                nc.vector.tensor_tensor(out=o, in0=o, in1=th[:], op=ALU.mult)
+                nc.sync.dma_start(out=out_block(out_0, t, j), in_=o)
+
+            for t in range(NT):
+                coef(t)
+            nc.scalar.dma_start(out=wc[:], in_=lnc_w1.partition_broadcast(P))
+            nc.scalar.dma_start(out=bc[:], in_=lnc_b1.partition_broadcast(P))
+            for t in range(NT + 1):
+                for s in range(NJ + 1):
+                    if t < NT and s < NJ:
+                        gates(t, s)
+                    if t < NT and s > 0:
+                        combine(t, s - 1)
+                    if t > 0 and s < NJ:
+                        finish(t - 1, s)
+                if t < NT:
+                    c_stats(t)

@@ -24,6 +24,8 @@ NJ = H // NBLK
 KP = H // 512
 NBUF = 3
 NWN = 3
+NPRE = 4
+NF32 = 2
 NBIG = 5
 WPAD = 144
 GN = 132
@@ -52,12 +54,20 @@ def tile_multilstm_pa_kernel(
         make_identity(nc, ident_b[:])
 
         wi_col = keep.tile([P, P], F32, name="wi_col")
-        w3t = keep.tile([P, NB, NBLK], F32, name="w3t")
+        w2t = keep.tile([P, NB - NF32, 2, NBLK], BF16, name="w2t")
+        w3f = keep.tile([P, NF32, NBLK], F32, name="w3f")
+        xt_f = keep.tile([P, NT, V], F32, name="xt_f")
+        csum = keep.tile([P, NT, NJ], F32, name="csum")
+        csq = keep.tile([P, NT, NJ], F32, name="csq")
+        nshift = keep.tile([P, NT, 1], F32, name="nshift")
+        cst = keep.tile([P, NT, 4], F32, name="cst")
         fo = keep.tile([P, NT, 2, NJ, NBLK], F32, name="fo")
         bnr = keep.tile([P, NT, NB, 6], F32, name="bnr")
-        bnc = keep.tile([P, NT, NJ, 6], F32, name="bnc")
         x_f = keep.tile([P, NT, V], F32, name="x_f")
-        xst = keep.tile([P, NT, V], F32, name="xst")
+        xt_b = keep.tile([P, NT, V], BF16, name="xt_b")
+        rstd_a = keep.tile([P, NT, 1], F32, name="rstd_a")
+        sig_a = keep.tile([P, NT, 1], F32, name="sig_a")
+        rho = keep.tile([P, NT, 1], F32, name="rho")
         cmat = keep.tile([P, NT, P], BF16, name="cmat")
         coeft = keep.tile([P, NT, P], BF16, name="coeft")
         mhalf = keep.tile([P, NT, 1], F32, name="mhalf")
@@ -96,7 +106,6 @@ def tile_multilstm_pa_kernel(
             for i in range(NWN):
                 nc.vector.memset(wnat[i][:], 1.0)
             nc.vector.memset(cmat[:], 0.0)
-            nc.vector.memset(cmat[:, :, 0:2], 1.0)
             nc.vector.memset(mhalf[:], -0.5)
 
             x_bf = one.tile([P, NT, V], BF16, name="x_bf")
@@ -111,8 +120,11 @@ def tile_multilstm_pa_kernel(
             xt_ps = psum.tile([P, NT, V], F32, tag="misc", bufs=2, name="xt_ps")
             for t in range(NT):
                 nc.tensor.transpose(xt_ps[:, t, :], x_f[:, t, :], ident_f[:])
-            xt_f = one.tile([P, NT, V], F32, name="xt_f")
             nc.vector.tensor_copy(out=xt_f[:], in_=xt_ps[:])
+            xb_ps = psum.tile([P, NT, V], BF16, tag="misc", bufs=2, name="xb_ps")
+            for t in range(NT):
+                nc.tensor.transpose(xb_ps[:, t, :], x_bf[:, t, :], ident_b[:])
+            nc.vector.tensor_copy(out=xt_b[:], in_=xb_ps[:])
 
             gram = psum.tile([P, GN], F32, tag="gram", bufs=1, name="gram")
 
@@ -122,20 +134,41 @@ def tile_multilstm_pa_kernel(
                     out=wn[:, :, 0:V],
                     in_=w_ih1[NBLK * b : NBLK * (b + 1), :].rearrange("(s p) k -> p s k", p=P),
                 )
-                w3n = one.tile([P, 4, V], F32, tag="w3n", bufs=2, name="w3n")
+                if b < NF32:
+                    w3n = one.tile([P, 4, V], F32, tag="w3n", bufs=1, name="w3n")
+                    for s in range(4):
+                        nc.tensor.matmul(
+                            out=gram[:], lhsT=wn[:, s, 0:V], rhs=wn[:, s, 0:GN],
+                            start=(b == 0 and s == 0), stop=(b == NB - 1 and s == 3),
+                        )
+                        nc.scalar.activation(
+                            out=w3n[:, s, :], in_=wn[:, s, 0:V], func=ACT.Copy,
+                            scale=wi_col[:, 4 * b + s : 4 * b + s + 1],
+                        )
+                    tf = psum.tile([P, NBLK], F32, tag="big", bufs=NBIG, name="tf")
+                    for s in range(4):
+                        nc.tensor.transpose(tf[:, V * s : V * (s + 1)], w3n[:, s, :], ident_f[:])
+                    nc.scalar.copy(out=w3f[:, b, :], in_=tf[:])
+                    return
+                hi = one.tile([P, 4, V], BF16, tag="w2hi", bufs=2, name="hi")
+                lo = one.tile([P, 4, V], BF16, tag="w2lo", bufs=2, name="lo")
                 for s in range(4):
+                    wi_s = wi_col[:, 4 * b + s : 4 * b + s + 1]
                     nc.tensor.matmul(
                         out=gram[:], lhsT=wn[:, s, 0:V], rhs=wn[:, s, 0:GN],
                         start=(b == 0 and s == 0), stop=(b == NB - 1 and s == 3),
                     )
-                    nc.scalar.activation(
-                        out=w3n[:, s, :], in_=wn[:, s, 0:V], func=ACT.Copy,
-                        scale=wi_col[:, 4 * b + s : 4 * b + s + 1],
+                    nc.scalar.activation(out=hi[:, s, :], in_=wn[:, s, 0:V], func=ACT.Copy, scale=wi_s)
+                    nc.vector.scalar_tensor_tensor(
+                        out=lo[:, s, :], in0=wn[:, s, 0:V], scalar=wi_s, in1=hi[:, s, :],
+                        op0=ALU.mult, op1=ALU.subtract,
                     )
-                tp = psum.tile([P, NBLK], F32, tag="big", bufs=NBIG, name="tp")
+                tp = psum.tile([P, 2, NBLK], BF16, tag="big", bufs=NBIG, name="tp")
                 for s in range(4):
-                    nc.tensor.transpose(tp[:, V * s : V * (s + 1)], w3n[:, s, :], ident_f[:])
-                nc.scalar.copy(out=w3t[:, b, :], in_=tp[:])
+                    nc.tensor.transpose(tp[:, 0, V * s : V * (s + 1)], hi[:, s, :], ident_b[:])
+                for s in range(4):
+                    nc.tensor.transpose(tp[:, 1, V * s : V * (s + 1)], lo[:, s, :], ident_b[:])
+                nc.scalar.copy(out=w2t[:, b - NF32, :, :], in_=tp[:])
 
             def a_stats():
                 gs = one.tile([P, GN], F32, name="gs")
@@ -159,21 +192,17 @@ def tile_multilstm_pa_kernel(
                     out=var_a[:], in0=ssq[:], scalar=1.0 / G, in1=msq[:], op0=ALU.mult, op1=ALU.subtract,
                 )
                 nc.gpsimd.tensor_single_scalar(out=var_a[:], in_=var_a[:], scalar=EPS, op=ALU.add)
-                rstd_a = one.tile([P, NT, 1], F32, name="rstd_a")
                 nc.gpsimd.tensor_tensor(out=rstd_a[:], in0=var_a[:], in1=mhalf[:], op=ALU.pow)
+                nc.vector.tensor_tensor(out=sig_a[:], in0=var_a[:], in1=rstd_a[:], op=ALU.mult)
                 negma = one.tile([P, NT, 1], F32, name="negma")
-                nc.vector.scalar_tensor_tensor(
-                    out=negma[:], in0=mean_a[:], scalar=-1.0, in1=rstd_a[:], op0=ALU.mult, op1=ALU.mult,
-                )
+                nc.vector.tensor_single_scalar(out=negma[:], in_=mean_a[:], scalar=-1.0, op=ALU.mult)
                 rem_a = one.tile([P, NT, 2], F32, name="rem_a")
-                split3(negma[:], rem_a, cmat, 5)
-                xs = one.tile([P, NT, V], F32, name="xs")
-                xs_ps = psum.tile([P, NT, V], F32, tag="misc", bufs=2, name="xs_ps")
-                for t in range(NT):
-                    nc.vector.tensor_scalar_mul(out=xs[:, t, :], in0=x_f[:, t, :], scalar1=rstd_a[:, t, :])
-                    nc.tensor.transpose(xs_ps[:, t, :], xs[:, t, :], ident_f[:])
-                nc.vector.tensor_copy(out=xst[:], in_=xs_ps[:])
+                split3(sig_a[:], rem_a, cmat, 0)
+                nc.vector.tensor_copy(out=cmat[:, :, 4:7], in_=cmat[:, :, 0:3])
+                split3(negma[:], rem_a, cmat, 8)
 
+            for b in range(NPRE):
+                make_w3(b)
             for b in range(NB):
                 cod, pl = wcod[b % NBUF], wpl[b % NBUF]
                 for q4 in range(4):
@@ -209,10 +238,10 @@ def tile_multilstm_pa_kernel(
                         stg = one.tile([P, NBLK], F32, tag="stg", bufs=3, name="stg")
                         nc.vector.tensor_tensor(out=stg[:], in0=acc[:], in1=whb[:], op=ALU.mult)
                         nc.gpsimd.dma_start(out=out_block(out_0 if q == 0 else out_1, t, j), in_=stg[:])
-                if b < NB // 2:
-                    make_w3(2 * b)
-                    make_w3(2 * b + 1)
-                if b == NB // 2:
+                if b < (NB - NPRE) // 2:
+                    make_w3(NPRE + 2 * b)
+                    make_w3(NPRE + 2 * b + 1)
+                if b == (NB - NPRE) // 2:
                     a_stats()
 
         with tc.tile_pool(name="tail", bufs=1) as tail:
@@ -226,11 +255,12 @@ def tile_multilstm_pa_kernel(
                 nc.vector.bn_aggr(out=mvr[:, t, :], in_=bnr[:, t, :, :].rearrange("p b s -> p (b s)"))
                 nc.gpsimd.tensor_single_scalar(out=ve_r[:, t, :], in_=mvr[:, t, 1:2], scalar=EPS, op=ALU.add)
                 nc.gpsimd.tensor_tensor(out=rstd_r[:, t, :], in0=ve_r[:, t, :], in1=mhalf[:, t, :], op=ALU.pow)
+                nc.vector.tensor_tensor(out=rho[:, t, :], in0=rstd_r[:, t, :], in1=sig_a[:, t, :], op=ALU.mult)
                 nc.vector.scalar_tensor_tensor(
-                    out=negc[:, t, :], in0=mvr[:, t, 0:1], scalar=-1.0, in1=rstd_r[:, t, :],
+                    out=negc[:, t, :], in0=mvr[:, t, 0:1], scalar=-1.0, in1=rho[:, t, :],
                     op0=ALU.mult, op1=ALU.mult,
                 )
-                split3(negc[:, t : t + 1, :], rem_r[:, t : t + 1, :], cmat[:, t : t + 1, :], 2)
+                split3(negc[:, t : t + 1, :], rem_r[:, t : t + 1, :], cmat[:, t : t + 1, :], 12)
                 pc = psum.tile([P, P], BF16, tag="misc", bufs=2, name="pc")
                 nc.tensor.transpose(pc[:], cmat[:, t, :], ident_b[:])
                 nc.vector.tensor_copy(out=coeft[:, t, :], in_=pc[:])
@@ -242,10 +272,10 @@ def tile_multilstm_pa_kernel(
 
             def gates(t, j):
                 rw = rows[(t * NJ + j) % 2]
-                nc.sync.dma_start(out=rw[0:1, :, :], in_=vec_rows(lni_b1, j, 1))
-                nc.sync.dma_start(out=rw[1:2, :, :], in_=vec_rows(lnh_b1, j, 1))
-                nc.sync.dma_start(out=rw[2:5, :, :], in_=vec_rows(lnh_w1, j, 3))
-                nc.sync.dma_start(out=rw[5:8, :, :], in_=vec_rows(lni_w1, j, 3))
+                nc.sync.dma_start(out=rw[0:4, :, :], in_=vec_rows(lni_b1, j, 4))
+                nc.sync.dma_start(out=rw[4:8, :, :], in_=vec_rows(lnh_b1, j, 4))
+                nc.sync.dma_start(out=rw[8:12, :, :], in_=vec_rows(lni_w1, j, 4))
+                nc.sync.dma_start(out=rw[12:16, :, :], in_=vec_rows(lnh_w1, j, 4))
                 ri = tail.tile([P, NBLK], F32, tag="rb", bufs=8, name="ri")
                 nc.sync.dma_start(out=ri[:], in_=out_block(out_0, t, j))
                 rg = tail.tile([P, NBLK], F32, tag="rb", bufs=8, name="rg")
@@ -255,23 +285,46 @@ def tile_multilstm_pa_kernel(
                 live[(t, j)] = (ri, rg, c0b)
                 for q, chunk in ((0, ri[:]), (2, rg[:]), (1, fo[:, t, 0, j, :]), (3, fo[:, t, 1, j, :])):
                     pg = psum.tile([P, NBLK], F32, tag="big", bufs=NBIG, name="pg")
-                    nc.tensor.matmul(out=pg[:], lhsT=xst[:, t, :], rhs=w3t[:, NJ * q + j, :], start=True, stop=False)
+                    b = NJ * q + j
+                    if b < NF32:
+                        nc.tensor.matmul(out=pg[:], lhsT=xt_f[:, t, :], rhs=w3f[:, b, :], start=True, stop=False)
+                    else:
+                        nc.tensor.matmul(out=pg[:], lhsT=xt_b[:, t, :], rhs=w2t[:, b - NF32, 0, :], start=True, stop=False)
+                        nc.tensor.matmul(out=pg[:], lhsT=xt_b[:, t, :], rhs=w2t[:, b - NF32, 1, :], start=False, stop=False)
                     nc.tensor.matmul(out=pg[:], lhsT=coeft[:, t, :], rhs=rw[:, q, :], start=False, stop=True)
                     nc.vector.scalar_tensor_tensor(
-                        out=chunk, in0=chunk, scalar=rstd_r[:, t, :], in1=pg[:], op0=ALU.mult, op1=ALU.add,
+                        out=chunk, in0=chunk, scalar=rho[:, t, :], in1=pg[:], op0=ALU.mult, op1=ALU.add,
                     )
-                    nc.scalar.activation(out=chunk, in_=chunk, func=(ACT.Tanh if q == 2 else ACT.Sigmoid))
+                    nc.scalar.activation(
+                        out=chunk, in_=chunk, func=(ACT.Tanh if q == 2 else ACT.Sigmoid), scale=rstd_a[:, t, :],
+                    )
 
             def combine(t, j):
                 ri, rg, c0b = live[(t, j)]
                 f = fo[:, t, 0, j, :]
                 nc.vector.tensor_tensor(out=ri[:], in0=ri[:], in1=rg[:], op=ALU.mult)
                 nc.vector.tensor_tensor(out=f, in0=f, in1=c0b[:], op=ALU.mult)
-                nc.vector.tensor_tensor(out=f, in0=f, in1=ri[:], op=ALU.add)
-                nc.vector.bn_stats(out=bnc[:, t, j, :], in_=f)
+                nc.vector.scalar_tensor_tensor(
+                    out=f, in0=f, scalar=1.0, in1=ri[:], op0=ALU.mult, op1=ALU.add, accum_out=csum[:, t, j : j + 1],
+                )
+                if j == 0:
+                    nc.vector.tensor_single_scalar(
+                        out=nshift[:, t, :], in_=csum[:, t, 0:1], scalar=-1.0 / NBLK, op=ALU.mult,
+                    )
+                nc.scalar.activation(
+                    out=rg[:], in_=f, func=ACT.Square, bias=nshift[:, t, :], accum_out=csq[:, t, j : j + 1],
+                )
 
             def c_stats(t):
-                nc.vector.bn_aggr(out=mvc[:, t, :], in_=bnc[:, t, :, :].rearrange("p b s -> p (b s)"))
+                nc.vector.tensor_reduce(out=cst[:, t, 0:1], in_=csum[:, t, :], axis=mybir.AxisListType.X, op=ALU.add)
+                nc.vector.tensor_reduce(out=cst[:, t, 1:2], in_=csq[:, t, :], axis=mybir.AxisListType.X, op=ALU.add)
+                nc.vector.tensor_single_scalar(out=mvc[:, t, 0:1], in_=cst[:, t, 0:1], scalar=1.0 / H, op=ALU.mult)
+                nc.vector.tensor_tensor(out=cst[:, t, 2:3], in0=mvc[:, t, 0:1], in1=nshift[:, t, :], op=ALU.add)
+                nc.vector.tensor_tensor(out=cst[:, t, 3:4], in0=cst[:, t, 2:3], in1=cst[:, t, 2:3], op=ALU.mult)
+                nc.vector.scalar_tensor_tensor(
+                    out=mvc[:, t, 1:2], in0=cst[:, t, 1:2], scalar=1.0 / H, in1=cst[:, t, 3:4],
+                    op0=ALU.mult, op1=ALU.subtract,
+                )
                 nc.gpsimd.tensor_single_scalar(out=ve_c[:, t, :], in_=mvc[:, t, 1:2], scalar=EPS, op=ALU.add)
                 nc.gpsimd.tensor_tensor(out=rstd_c[:, t, :], in0=ve_c[:, t, :], in1=mhalf[:, t, :], op=ALU.pow)
 

@@ -10,6 +10,7 @@ I32 = mybir.dt.int32
 FP4X4 = mybir.dt.float4_e2m1fn_x4
 ALU = mybir.AluOpType
 ACT = mybir.ActivationFunctionType
+AX = mybir.AxisListType
 
 B, V, H = 384, 128, 4096
 G = 4 * H
@@ -24,9 +25,8 @@ NJ = H // NBLK
 KP = H // 512
 NBUF = 3
 NWN = 3
-NPRE = 4
-NF32 = 2
 NBIG = 5
+NF32 = 2
 WPAD = 144
 GN = 132
 
@@ -48,28 +48,24 @@ def tile_multilstm_pa_kernel(
         nc.vector.memset(warm[:], 0.0)
         nc.scalar.activation(out=warm[:], in_=warm[:], func=ACT.Sigmoid)
 
-        ident_f = keep.tile([P, P], F32, name="ident_f")
-        make_identity(nc, ident_f[:])
         ident_b = keep.tile([P, P], BF16, name="ident_b")
         make_identity(nc, ident_b[:])
+        ident_f = keep.tile([P, P], F32, name="ident_f")
+        make_identity(nc, ident_f[:])
 
-        wi_col = keep.tile([P, P], F32, name="wi_col")
         w2t = keep.tile([P, NB - NF32, 2, NBLK], BF16, name="w2t")
         w3f = keep.tile([P, NF32, NBLK], F32, name="w3f")
-        xt_f = keep.tile([P, NT, V], F32, name="xt_f")
-        csum = keep.tile([P, NT, NJ], F32, name="csum")
-        csq = keep.tile([P, NT, NJ], F32, name="csq")
-        nshift = keep.tile([P, NT, 1], F32, name="nshift")
-        cst = keep.tile([P, NT, 4], F32, name="cst")
-        fo = keep.tile([P, NT, 2, NJ, NBLK], F32, name="fo")
-        bnr = keep.tile([P, NT, NB, 6], F32, name="bnr")
-        x_f = keep.tile([P, NT, V], F32, name="x_f")
         xt_b = keep.tile([P, NT, V], BF16, name="xt_b")
-        rstd_a = keep.tile([P, NT, 1], F32, name="rstd_a")
-        sig_a = keep.tile([P, NT, 1], F32, name="sig_a")
-        rho = keep.tile([P, NT, 1], F32, name="rho")
-        cmat = keep.tile([P, NT, P], BF16, name="cmat")
-        coeft = keep.tile([P, NT, P], BF16, name="coeft")
+        xt_f = keep.tile([P, NT, V], F32, name="xt_f")
+        fo = keep.tile([P, NT, NJ, 2, NBLK], F32, name="fo")
+        bnr = keep.tile([P, NT, NB, 6], F32, name="bnr")
+        cmat = keep.tile([P, NT, 16], BF16, name="cmat")
+        mask = keep.tile([P, NJ], F32, name="mask")
+        nc.vector.tensor_reduce(
+            out=mask[:], in_=ident_b[:].rearrange("p (j c) -> p j c", c=16), axis=AX.X, op=ALU.add,
+        )
+        coeft = keep.tile([P, NT, NJ, P], BF16, name="coeft")
+        rows = keep.tile([P, 4, NBLK], BF16, name="rows")
         mhalf = keep.tile([P, NT, 1], F32, name="mhalf")
         mvr = keep.tile([P, NT, 2], F32, name="mvr")
         mvc = keep.tile([P, NT, 2], F32, name="mvc")
@@ -77,8 +73,17 @@ def tile_multilstm_pa_kernel(
         ve_c = keep.tile([P, NT, 1], F32, name="ve_c")
         rstd_r = keep.tile([P, NT, 1], F32, name="rstd_r")
         rstd_c = keep.tile([P, NT, 1], F32, name="rstd_c")
+        rstd_a = keep.tile([P, NT, 1], F32, name="rstd_a")
+        sig_a = keep.tile([P, NT, 1], F32, name="sig_a")
+        rho = keep.tile([P, NT, 1], F32, name="rho")
         negc = keep.tile([P, NT, 1], F32, name="negc")
         rem_r = keep.tile([P, NT, 2], F32, name="rem_r")
+        csum = keep.tile([P, NT, NJ], F32, name="csum")
+        csq = keep.tile([P, NT, NJ], F32, name="csq")
+        nshift = keep.tile([P, NT, 1], F32, name="nshift")
+        cst = keep.tile([P, NT, 4], F32, name="cst")
+        nc.vector.memset(cmat[:], 0.0)
+        nc.vector.memset(mhalf[:], -0.5)
 
         def split3(src, rem, cm, col):
             nc.vector.tensor_copy(out=cm[:, :, col : col + 1], in_=src)
@@ -86,6 +91,24 @@ def tile_multilstm_pa_kernel(
             nc.vector.tensor_copy(out=cm[:, :, col + 1 : col + 2], in_=rem[:, :, 0:1])
             nc.vector.tensor_tensor(out=rem[:, :, 1:2], in0=rem[:, :, 0:1], in1=cm[:, :, col + 1 : col + 2], op=ALU.subtract)
             nc.vector.tensor_copy(out=cm[:, :, col + 2 : col + 3], in_=rem[:, :, 1:2])
+
+        def coef(t):
+            nc.vector.bn_aggr(out=mvr[:, t, :], in_=bnr[:, t, :, :].rearrange("p b s -> p (b s)"))
+            nc.gpsimd.tensor_single_scalar(out=ve_r[:, t, :], in_=mvr[:, t, 1:2], scalar=EPS, op=ALU.add)
+            nc.gpsimd.tensor_tensor(out=rstd_r[:, t, :], in0=ve_r[:, t, :], in1=mhalf[:, t, :], op=ALU.pow)
+            nc.vector.tensor_tensor(out=rho[:, t, :], in0=rstd_r[:, t, :], in1=sig_a[:, t, :], op=ALU.mult)
+            nc.vector.scalar_tensor_tensor(
+                out=negc[:, t, :], in0=mvr[:, t, 0:1], scalar=-1.0, in1=rho[:, t, :], op0=ALU.mult, op1=ALU.mult,
+            )
+            split3(negc[:, t : t + 1, :], rem_r[:, t : t + 1, :], cmat[:, t : t + 1, :], 12)
+            crep = keep.tile([P, NJ, 16], BF16, tag="crep", bufs=2, name="crep")
+            nc.vector.tensor_copy(out=crep[:], in_=cmat[:, t : t + 1, :].to_broadcast([P, NJ, 16]))
+            pc = psum.tile([P, P], BF16, tag="misc", bufs=2, name="pc")
+            nc.tensor.transpose(pc[:], crep[:].rearrange("p j c -> p (j c)"), ident_b[:])
+            nc.vector.tensor_tensor(
+                out=coeft[:, t, :, :], in0=pc[:].unsqueeze(1).to_broadcast([P, NJ, P]),
+                in1=mask[:].unsqueeze(2).to_broadcast([P, NJ, P]), op=ALU.mult,
+            )
 
         with tc.tile_pool(name="stream", bufs=1) as one:
             h0c = one.tile([P, KP, 2 * B], U8, name="h0c", align_bytes=64)
@@ -105,18 +128,17 @@ def tile_multilstm_pa_kernel(
                 )
             for i in range(NWN):
                 nc.vector.memset(wnat[i][:], 1.0)
-            nc.vector.memset(cmat[:], 0.0)
-            nc.vector.memset(mhalf[:], -0.5)
 
             x_bf = one.tile([P, NT, V], BF16, name="x_bf")
             nc.scalar.dma_start(out=x_bf[:], in_=x.rearrange("(t p) k -> p t k", p=P))
+            x_f = one.tile([P, NT, V], F32, name="x_f")
             nc.vector.tensor_copy(out=x_f[:], in_=x_bf[:])
             wi_nat = one.tile([P, P], BF16, name="wi_nat")
             nc.scalar.dma_start(out=wi_nat[:], in_=lni_w1.rearrange("(c p) -> c p", p=P))
+            wi_col = one.tile([P, P], F32, name="wi_col")
             wi_ps = psum.tile([P, P], BF16, tag="misc", bufs=2, name="wi_ps")
             nc.tensor.transpose(wi_ps[:], wi_nat[:], ident_b[:])
             nc.vector.tensor_copy(out=wi_col[:], in_=wi_ps[:])
-
             xt_ps = psum.tile([P, NT, V], F32, tag="misc", bufs=2, name="xt_ps")
             for t in range(NT):
                 nc.tensor.transpose(xt_ps[:, t, :], x_f[:, t, :], ident_f[:])
@@ -126,49 +148,37 @@ def tile_multilstm_pa_kernel(
                 nc.tensor.transpose(xb_ps[:, t, :], x_bf[:, t, :], ident_b[:])
             nc.vector.tensor_copy(out=xt_b[:], in_=xb_ps[:])
 
+            for v, vec in enumerate((lni_b1, lnh_b1, lni_w1, lnh_w1)):
+                for i in range(4):
+                    nc.scalar.dma_start(
+                        out=rows[4 * v + i : P : 16, :, :], in_=vec.rearrange("(q j n) -> j q n", q=4, j=NJ),
+                    )
+
             gram = psum.tile([P, GN], F32, tag="gram", bufs=1, name="gram")
 
-            def make_w3(b):
+            def make_w2(b):
                 wn = wnat[b % NWN]
                 nc.scalar.dma_start(
                     out=wn[:, :, 0:V],
                     in_=w_ih1[NBLK * b : NBLK * (b + 1), :].rearrange("(s p) k -> p s k", p=P),
                 )
-                if b < NF32:
-                    w3n = one.tile([P, 4, V], F32, tag="w3n", bufs=1, name="w3n")
-                    for s in range(4):
-                        nc.tensor.matmul(
-                            out=gram[:], lhsT=wn[:, s, 0:V], rhs=wn[:, s, 0:GN],
-                            start=(b == 0 and s == 0), stop=(b == NB - 1 and s == 3),
-                        )
-                        nc.scalar.activation(
-                            out=w3n[:, s, :], in_=wn[:, s, 0:V], func=ACT.Copy,
-                            scale=wi_col[:, 4 * b + s : 4 * b + s + 1],
-                        )
-                    tf = psum.tile([P, NBLK], F32, tag="big", bufs=NBIG, name="tf")
-                    for s in range(4):
-                        nc.tensor.transpose(tf[:, V * s : V * (s + 1)], w3n[:, s, :], ident_f[:])
-                    nc.scalar.copy(out=w3f[:, b, :], in_=tf[:])
-                    return
-                hi = one.tile([P, 4, V], BF16, tag="w2hi", bufs=2, name="hi")
-                lo = one.tile([P, 4, V], BF16, tag="w2lo", bufs=2, name="lo")
                 for s in range(4):
+                    cols = slice(V * s, V * (s + 1))
                     wi_s = wi_col[:, 4 * b + s : 4 * b + s + 1]
                     nc.tensor.matmul(
                         out=gram[:], lhsT=wn[:, s, 0:V], rhs=wn[:, s, 0:GN],
                         start=(b == 0 and s == 0), stop=(b == NB - 1 and s == 3),
                     )
-                    nc.scalar.activation(out=hi[:, s, :], in_=wn[:, s, 0:V], func=ACT.Copy, scale=wi_s)
-                    nc.vector.scalar_tensor_tensor(
-                        out=lo[:, s, :], in0=wn[:, s, 0:V], scalar=wi_s, in1=hi[:, s, :],
-                        op0=ALU.mult, op1=ALU.subtract,
-                    )
-                tp = psum.tile([P, 2, NBLK], BF16, tag="big", bufs=NBIG, name="tp")
-                for s in range(4):
-                    nc.tensor.transpose(tp[:, 0, V * s : V * (s + 1)], hi[:, s, :], ident_b[:])
-                for s in range(4):
-                    nc.tensor.transpose(tp[:, 1, V * s : V * (s + 1)], lo[:, s, :], ident_b[:])
-                nc.scalar.copy(out=w2t[:, b - NF32, :, :], in_=tp[:])
+                    if b < NF32:
+                        nc.scalar.activation(out=w3f[:, b, cols], in_=wn[:, s, 0:V], func=ACT.Copy, scale=wi_s)
+                    else:
+                        nc.scalar.activation(
+                            out=w2t[:, b - NF32, 0, cols], in_=wn[:, s, 0:V], func=ACT.Copy, scale=wi_s,
+                        )
+                        nc.vector.scalar_tensor_tensor(
+                            out=w2t[:, b - NF32, 1, cols], in0=wn[:, s, 0:V], scalar=wi_s,
+                            in1=w2t[:, b - NF32, 0, cols], op0=ALU.mult, op1=ALU.subtract,
+                        )
 
             def a_stats():
                 gs = one.tile([P, GN], F32, name="gs")
@@ -201,8 +211,6 @@ def tile_multilstm_pa_kernel(
                 nc.vector.tensor_copy(out=cmat[:, :, 4:7], in_=cmat[:, :, 0:3])
                 split3(negma[:], rem_a, cmat, 8)
 
-            for b in range(NPRE):
-                make_w3(b)
             for b in range(NB):
                 cod, pl = wcod[b % NBUF], wpl[b % NBUF]
                 for q4 in range(4):
@@ -217,7 +225,6 @@ def tile_multilstm_pa_kernel(
                 )
                 whb = one.tile([P, NBLK], BF16, tag="whb", bufs=3, name="whb")
                 nc.sync.dma_start(out=whb[:], in_=lnh_w1[NBLK * b : NBLK * (b + 1)].partition_broadcast(P))
-
                 q, j = b // NJ, b % NJ
                 for t in range(NT):
                     acc = psum.tile([P, NBLK], F32, tag="big", bufs=NBIG, name="acc")
@@ -233,57 +240,60 @@ def tile_multilstm_pa_kernel(
                         )
                     nc.vector.bn_stats(out=bnr[:, t, b, :], in_=acc[:])
                     if q % 2 == 1:
-                        nc.vector.tensor_tensor(out=fo[:, t, q // 2, j, :], in0=acc[:], in1=whb[:], op=ALU.mult)
+                        nc.vector.tensor_tensor(out=fo[:, t, j, q // 2, :], in0=acc[:], in1=whb[:], op=ALU.mult)
                     else:
                         stg = one.tile([P, NBLK], F32, tag="stg", bufs=3, name="stg")
                         nc.vector.tensor_tensor(out=stg[:], in0=acc[:], in1=whb[:], op=ALU.mult)
                         nc.gpsimd.dma_start(out=out_block(out_0 if q == 0 else out_1, t, j), in_=stg[:])
-                if b < (NB - NPRE) // 2:
-                    make_w3(NPRE + 2 * b)
-                    make_w3(NPRE + 2 * b + 1)
-                if b == (NB - NPRE) // 2:
+                    if b == NB - 1:
+                        coef(t)
+                if b < NB // 2:
+                    make_w2(2 * b)
+                    make_w2(2 * b + 1)
+                if b == NB // 2:
                     a_stats()
 
         with tc.tile_pool(name="tail", bufs=1) as tail:
-            rows = [tail.tile([P, 4, NBLK], BF16, name="rows%d" % i) for i in range(2)]
-            for i in range(2):
-                nc.gpsimd.memset(rows[i][:], 0.0)
             wc = tail.tile([P, H], BF16, name="wc")
             bc = tail.tile([P, H], BF16, name="bc")
 
-            def coef(t):
-                nc.vector.bn_aggr(out=mvr[:, t, :], in_=bnr[:, t, :, :].rearrange("p b s -> p (b s)"))
-                nc.gpsimd.tensor_single_scalar(out=ve_r[:, t, :], in_=mvr[:, t, 1:2], scalar=EPS, op=ALU.add)
-                nc.gpsimd.tensor_tensor(out=rstd_r[:, t, :], in0=ve_r[:, t, :], in1=mhalf[:, t, :], op=ALU.pow)
-                nc.vector.tensor_tensor(out=rho[:, t, :], in0=rstd_r[:, t, :], in1=sig_a[:, t, :], op=ALU.mult)
-                nc.vector.scalar_tensor_tensor(
-                    out=negc[:, t, :], in0=mvr[:, t, 0:1], scalar=-1.0, in1=rho[:, t, :],
-                    op0=ALU.mult, op1=ALU.mult,
-                )
-                split3(negc[:, t : t + 1, :], rem_r[:, t : t + 1, :], cmat[:, t : t + 1, :], 12)
-                pc = psum.tile([P, P], BF16, tag="misc", bufs=2, name="pc")
-                nc.tensor.transpose(pc[:], cmat[:, t, :], ident_b[:])
-                nc.vector.tensor_copy(out=coeft[:, t, :], in_=pc[:])
-
             live = {}
+            pending = []
 
-            def vec_rows(vec, j, n):
-                return vec.rearrange("(q j n) -> q j n", q=4, j=NJ)[:, j, :].partition_broadcast(n)
+            units = [(t, j) for j in range(NJ) for t in range(NT)]
 
-            def gates(t, j):
-                rw = rows[(t * NJ + j) % 2]
-                nc.sync.dma_start(out=rw[0:4, :, :], in_=vec_rows(lni_b1, j, 4))
-                nc.sync.dma_start(out=rw[4:8, :, :], in_=vec_rows(lnh_b1, j, 4))
-                nc.sync.dma_start(out=rw[8:12, :, :], in_=vec_rows(lni_w1, j, 4))
-                nc.sync.dma_start(out=rw[12:16, :, :], in_=vec_rows(lnh_w1, j, 4))
+            def fetch(u):
+                t, j = units[u]
                 ri = tail.tile([P, NBLK], F32, tag="rb", bufs=8, name="ri")
                 nc.sync.dma_start(out=ri[:], in_=out_block(out_0, t, j))
                 rg = tail.tile([P, NBLK], F32, tag="rb", bufs=8, name="rg")
                 nc.sync.dma_start(out=rg[:], in_=out_block(out_1, t, j))
-                c0b = tail.tile([P, NBLK], BF16, tag="c0b", bufs=3, name="c0b")
+                c0b = tail.tile([P, NBLK], BF16, tag="c0b", bufs=4, name="c0b")
                 nc.sync.dma_start(out=c0b[:], in_=out_block(c0, t, j))
                 live[(t, j)] = (ri, rg, c0b)
-                for q, chunk in ((0, ri[:]), (2, rg[:]), (1, fo[:, t, 0, j, :]), (3, fo[:, t, 1, j, :])):
+
+            def turn(b, by_scalar):
+                if b < NF32:
+                    tp = psum.tile([P, NBLK], F32, tag="big", bufs=NBIG, name="tf")
+                    for s in range(4):
+                        nc.tensor.transpose(tp[:, V * s : V * (s + 1)], w3f[:, b, V * s : V * (s + 1)], ident_f[:])
+                    dst = w3f[:, b, :]
+                else:
+                    tp = psum.tile([P, 2, NBLK], BF16, tag="big", bufs=NBIG, name="tp")
+                    for h in range(2):
+                        for s in range(4):
+                            nc.tensor.transpose(
+                                tp[:, h, V * s : V * (s + 1)], w2t[:, b - NF32, h, V * s : V * (s + 1)], ident_b[:],
+                            )
+                    dst = w2t[:, b - NF32, :, :]
+                if by_scalar:
+                    nc.scalar.copy(out=dst, in_=tp[:])
+                else:
+                    nc.vector.tensor_copy(out=dst, in_=tp[:])
+
+            def gates(t, j):
+                ri, rg, c0b = live[(t, j)]
+                for q, chunk in ((0, ri[:]), (2, rg[:]), (1, fo[:, t, j, 0, :]), (3, fo[:, t, j, 1, :])):
                     pg = psum.tile([P, NBLK], F32, tag="big", bufs=NBIG, name="pg")
                     b = NJ * q + j
                     if b < NF32:
@@ -291,7 +301,7 @@ def tile_multilstm_pa_kernel(
                     else:
                         nc.tensor.matmul(out=pg[:], lhsT=xt_b[:, t, :], rhs=w2t[:, b - NF32, 0, :], start=True, stop=False)
                         nc.tensor.matmul(out=pg[:], lhsT=xt_b[:, t, :], rhs=w2t[:, b - NF32, 1, :], start=False, stop=False)
-                    nc.tensor.matmul(out=pg[:], lhsT=coeft[:, t, :], rhs=rw[:, q, :], start=False, stop=True)
+                    nc.tensor.matmul(out=pg[:], lhsT=coeft[:, t, j, :], rhs=rows[:, q, :], start=False, stop=True)
                     nc.vector.scalar_tensor_tensor(
                         out=chunk, in0=chunk, scalar=rho[:, t, :], in1=pg[:], op0=ALU.mult, op1=ALU.add,
                     )
@@ -301,7 +311,7 @@ def tile_multilstm_pa_kernel(
 
             def combine(t, j):
                 ri, rg, c0b = live[(t, j)]
-                f = fo[:, t, 0, j, :]
+                f = fo[:, t, j, 0, :]
                 nc.vector.tensor_tensor(out=ri[:], in0=ri[:], in1=rg[:], op=ALU.mult)
                 nc.vector.tensor_tensor(out=f, in0=f, in1=c0b[:], op=ALU.mult)
                 nc.vector.scalar_tensor_tensor(
@@ -316,8 +326,8 @@ def tile_multilstm_pa_kernel(
                 )
 
             def c_stats(t):
-                nc.vector.tensor_reduce(out=cst[:, t, 0:1], in_=csum[:, t, :], axis=mybir.AxisListType.X, op=ALU.add)
-                nc.vector.tensor_reduce(out=cst[:, t, 1:2], in_=csq[:, t, :], axis=mybir.AxisListType.X, op=ALU.add)
+                nc.vector.tensor_reduce(out=cst[:, t, 0:1], in_=csum[:, t, :], axis=AX.X, op=ALU.add)
+                nc.vector.tensor_reduce(out=cst[:, t, 1:2], in_=csq[:, t, :], axis=AX.X, op=ALU.add)
                 nc.vector.tensor_single_scalar(out=mvc[:, t, 0:1], in_=cst[:, t, 0:1], scalar=1.0 / H, op=ALU.mult)
                 nc.vector.tensor_tensor(out=cst[:, t, 2:3], in0=mvc[:, t, 0:1], in1=nshift[:, t, :], op=ALU.add)
                 nc.vector.tensor_tensor(out=cst[:, t, 3:4], in0=cst[:, t, 2:3], in1=cst[:, t, 2:3], op=ALU.mult)
@@ -328,8 +338,13 @@ def tile_multilstm_pa_kernel(
                 nc.gpsimd.tensor_single_scalar(out=ve_c[:, t, :], in_=mvc[:, t, 1:2], scalar=EPS, op=ALU.add)
                 nc.gpsimd.tensor_tensor(out=rstd_c[:, t, :], in0=ve_c[:, t, :], in1=mhalf[:, t, :], op=ALU.pow)
 
+            def store_hy(queue):
+                for t, j in pending:
+                    queue.dma_start(out=out_block(out_0, t, j), in_=fo[:, t, j, 1, :])
+                pending.clear()
+
             def finish(t, j):
-                f, o = fo[:, t, 0, j, :], fo[:, t, 1, j, :]
+                f, o = fo[:, t, j, 0, :], fo[:, t, j, 1, :]
                 cols = slice(NBLK * j, NBLK * (j + 1))
                 nc.vector.scalar_tensor_tensor(
                     out=f, in0=f, scalar=mvc[:, t, 0:1], in1=wc[:, cols], op0=ALU.subtract, op1=ALU.mult,
@@ -340,20 +355,31 @@ def tile_multilstm_pa_kernel(
                 th = tail.tile([P, NBLK], F32, tag="th", bufs=2, name="th")
                 nc.scalar.activation(out=th[:], in_=f, func=ACT.Tanh)
                 nc.scalar.dma_start(out=out_block(out_1, t, j), in_=f)
+                store_hy(nc.scalar)
                 nc.vector.tensor_tensor(out=o, in0=o, in1=th[:], op=ALU.mult)
-                nc.sync.dma_start(out=out_block(out_0, t, j), in_=o)
+                pending.append((t, j))
 
+            fetch(0)
+            fetch(1)
+            nc.sync.dma_start(out=wc[:], in_=lnc_w1.partition_broadcast(P))
+            nc.sync.dma_start(out=bc[:], in_=lnc_b1.partition_broadcast(P))
+            for q in range(4):
+                turn(NJ * q, q % 2 == 0)
+            for u in range(len(units) + 1):
+                if u < len(units):
+                    t, j = units[u]
+                    if t == 0 and j + 1 < NJ:
+                        for q in range(4):
+                            turn(NJ * q + j + 1, q % 2 == 0)
+                    if u + 2 < len(units):
+                        fetch(u + 2)
+                    gates(t, j)
+                if u > 0:
+                    t, j = units[u - 1]
+                    combine(t, j)
+                    if j == NJ - 1:
+                        c_stats(t)
             for t in range(NT):
-                coef(t)
-            nc.scalar.dma_start(out=wc[:], in_=lnc_w1.partition_broadcast(P))
-            nc.scalar.dma_start(out=bc[:], in_=lnc_b1.partition_broadcast(P))
-            for t in range(NT + 1):
-                for s in range(NJ + 1):
-                    if t < NT and s < NJ:
-                        gates(t, s)
-                    if t < NT and s > 0:
-                        combine(t, s - 1)
-                    if t > 0 and s < NJ:
-                        finish(t - 1, s)
-                if t < NT:
-                    c_stats(t)
+                for j in range(NJ):
+                    finish(t, j)
+            store_hy(nc.sync)

@@ -66,6 +66,7 @@ def tile_multilstm_pa_kernel(
         )
         coeft = keep.tile([P, NT, NJ, P], BF16, name="coeft")
         rows = keep.tile([P, 4, NBLK], BF16, name="rows")
+        cb_col = keep.tile([P, P], BF16, name="cb_col")
         mhalf = keep.tile([P, NT, 1], F32, name="mhalf")
         mvr = keep.tile([P, NT, 2], F32, name="mvr")
         mvc = keep.tile([P, NT, 2], F32, name="mvc")
@@ -139,6 +140,19 @@ def tile_multilstm_pa_kernel(
             wi_ps = psum.tile([P, P], BF16, tag="misc", bufs=2, name="wi_ps")
             nc.tensor.transpose(wi_ps[:], wi_nat[:], ident_b[:])
             nc.vector.tensor_copy(out=wi_col[:], in_=wi_ps[:])
+            wh_nat = one.tile([P, P], BF16, name="wh_nat")
+            nc.scalar.dma_start(out=wh_nat[:], in_=lnh_w1.rearrange("(c p) -> c p", p=P))
+            wh_col = one.tile([P, P], BF16, name="wh_col")
+            wh_ps = psum.tile([P, P], BF16, tag="misc", bufs=2, name="wh_ps")
+            nc.tensor.transpose(wh_ps[:], wh_nat[:], ident_b[:])
+            nc.vector.tensor_copy(out=wh_col[:], in_=wh_ps[:])
+            cb_nat = one.tile([P, P], BF16, name="cb_nat")
+            nc.vector.memset(cb_nat[:], 0.0)
+            nc.scalar.dma_start(out=cb_nat[0 : H // P, :], in_=lnc_w1.rearrange("(c p) -> c p", p=P))
+            nc.scalar.dma_start(out=cb_nat[H // P : 2 * H // P, :], in_=lnc_b1.rearrange("(c p) -> c p", p=P))
+            cb_ps = psum.tile([P, P], BF16, tag="misc", bufs=2, name="cb_ps")
+            nc.tensor.transpose(cb_ps[:], cb_nat[:], ident_b[:])
+            nc.vector.tensor_copy(out=cb_col[:], in_=cb_ps[:])
             xt_ps = psum.tile([P, NT, V], F32, tag="misc", bufs=2, name="xt_ps")
             for t in range(NT):
                 nc.tensor.transpose(xt_ps[:, t, :], x_f[:, t, :], ident_f[:])
@@ -223,8 +237,15 @@ def tile_multilstm_pa_kernel(
                     out=cod[:],
                     in_=w_hh1_words[:, :, 2 * NBLK * b : 2 * NBLK * (b + 1)].rearrange("g p n -> p g n"),
                 )
+                whp = psum.tile([P, NBLK], BF16, tag="misc", bufs=2, name="whp")
+                for s in range(4):
+                    nc.tensor.transpose(
+                        whp[:, P * s : P * (s + 1)],
+                        wh_col[:, 4 * b + s : 4 * b + s + 1].to_broadcast([P, P]),
+                        ident_b[:],
+                    )
                 whb = one.tile([P, NBLK], BF16, tag="whb", bufs=3, name="whb")
-                nc.sync.dma_start(out=whb[:], in_=lnh_w1[NBLK * b : NBLK * (b + 1)].partition_broadcast(P))
+                nc.scalar.copy(out=whb[:], in_=whp[:])
                 q, j = b // NJ, b % NJ
                 for t in range(NT):
                     acc = psum.tile([P, NBLK], F32, tag="big", bufs=NBIG, name="acc")
@@ -361,8 +382,14 @@ def tile_multilstm_pa_kernel(
 
             fetch(0)
             fetch(1)
-            nc.sync.dma_start(out=wc[:], in_=lnc_w1.partition_broadcast(P))
-            nc.sync.dma_start(out=bc[:], in_=lnc_b1.partition_broadcast(P))
+
+            def spread(dst, first, j):
+                sp = psum.tile([P, NBLK], BF16, tag="misc", bufs=2, name="sp")
+                for s in range(4):
+                    c = first + 4 * j + s
+                    nc.tensor.transpose(sp[:, P * s : P * (s + 1)], cb_col[:, c : c + 1].to_broadcast([P, P]), ident_b[:])
+                nc.scalar.copy(out=dst[:, NBLK * j : NBLK * (j + 1)], in_=sp[:])
+
             for q in range(4):
                 turn(NJ * q, q % 2 == 0)
             for u in range(len(units) + 1):
@@ -374,6 +401,11 @@ def tile_multilstm_pa_kernel(
                     if u + 2 < len(units):
                         fetch(u + 2)
                     gates(t, j)
+                    if u >= NJ:
+                        if u % 2 == 0:
+                            spread(wc, 0, (u - NJ) // 2)
+                        else:
+                            spread(bc, H // P, (u - NJ) // 2)
                 if u > 0:
                     t, j = units[u - 1]
                     combine(t, j)

@@ -29,6 +29,8 @@ NBIG = 5
 NF32 = 2
 WPAD = 144
 GN = 132
+NLAST = 2
+NHEAD = 4
 
 
 def tile_multilstm_pa_kernel(
@@ -130,6 +132,37 @@ def tile_multilstm_pa_kernel(
             for i in range(NWN):
                 nc.vector.memset(wnat[i][:], 1.0)
 
+            wh_nat = one.tile([P, P], BF16, name="wh_nat")
+            nc.scalar.dma_start(out=wh_nat[:], in_=lnh_w1.rearrange("(c p) -> c p", p=P))
+            wh_col = one.tile([P, P], BF16, name="wh_col")
+            wh_ps = psum.tile([P, P], BF16, tag="misc", bufs=2, name="wh_ps")
+            nc.tensor.transpose(wh_ps[:], wh_nat[:], ident_b[:])
+            nc.vector.tensor_copy(out=wh_col[:], in_=wh_ps[:])
+
+            wh_last = one.tile([P, 2 * NBLK], BF16, name="wh_last")
+
+            def wh_pair(c):
+                if c == NB // 2 - 1:
+                    return wh_last[:]
+                return fo[:, c // NJ, c % NJ, 1, :].bitcast(BF16)
+
+            def spread_wh(c, tag, bufs, by_scalar):
+                wp = psum.tile([P, 2 * NBLK], BF16, tag=tag, bufs=bufs, name="wp")
+                for s in range(8):
+                    nc.tensor.transpose(
+                        wp[:, P * s : P * (s + 1)], wh_col[:, 8 * c + s : 8 * c + s + 1].to_broadcast([P, P]), ident_b[:],
+                    )
+                if by_scalar:
+                    nc.scalar.copy(out=wh_pair(c), in_=wp[:])
+                else:
+                    nc.vector.tensor_copy(out=wh_pair(c), in_=wp[:])
+
+            for c in range(NHEAD):
+                if c < NBIG:
+                    spread_wh(c, "big", NBIG, c % 2 == 0)
+                else:
+                    spread_wh(c, "misc", 2, c % 2 == 0)
+
             x_bf = one.tile([P, NT, V], BF16, name="x_bf")
             nc.scalar.dma_start(out=x_bf[:], in_=x.rearrange("(t p) k -> p t k", p=P))
             x_f = one.tile([P, NT, V], F32, name="x_f")
@@ -140,12 +173,6 @@ def tile_multilstm_pa_kernel(
             wi_ps = psum.tile([P, P], BF16, tag="misc", bufs=2, name="wi_ps")
             nc.tensor.transpose(wi_ps[:], wi_nat[:], ident_b[:])
             nc.vector.tensor_copy(out=wi_col[:], in_=wi_ps[:])
-            wh_nat = one.tile([P, P], BF16, name="wh_nat")
-            nc.scalar.dma_start(out=wh_nat[:], in_=lnh_w1.rearrange("(c p) -> c p", p=P))
-            wh_col = one.tile([P, P], BF16, name="wh_col")
-            wh_ps = psum.tile([P, P], BF16, tag="misc", bufs=2, name="wh_ps")
-            nc.tensor.transpose(wh_ps[:], wh_nat[:], ident_b[:])
-            nc.vector.tensor_copy(out=wh_col[:], in_=wh_ps[:])
             cb_nat = one.tile([P, P], BF16, name="cb_nat")
             nc.vector.memset(cb_nat[:], 0.0)
             nc.scalar.dma_start(out=cb_nat[0 : H // P, :], in_=lnc_w1.rearrange("(c p) -> c p", p=P))
@@ -225,7 +252,7 @@ def tile_multilstm_pa_kernel(
                 nc.vector.tensor_copy(out=cmat[:, :, 4:7], in_=cmat[:, :, 0:3])
                 split3(negma[:], rem_a, cmat, 8)
 
-            for b in range(NB):
+            def load_w(b):
                 cod, pl = wcod[b % NBUF], wpl[b % NBUF]
                 for q4 in range(4):
                     nc.sync.dma_start(
@@ -237,42 +264,48 @@ def tile_multilstm_pa_kernel(
                     out=cod[:],
                     in_=w_hh1_words[:, :, 2 * NBLK * b : 2 * NBLK * (b + 1)].rearrange("g p n -> p g n"),
                 )
-                whp = psum.tile([P, NBLK], BF16, tag="misc", bufs=2, name="whp")
-                for s in range(4):
-                    nc.tensor.transpose(
-                        whp[:, P * s : P * (s + 1)],
-                        wh_col[:, 4 * b + s : 4 * b + s + 1].to_broadcast([P, P]),
-                        ident_b[:],
-                    )
-                whb = one.tile([P, NBLK], BF16, tag="whb", bufs=3, name="whb")
-                nc.scalar.copy(out=whb[:], in_=whp[:])
+
+            def group(b, t):
+                cod, pl = wcod[b % NBUF], wpl[b % NBUF]
+                whb = wh_pair(b // 2)[:, NBLK * (b % 2) : NBLK * (b % 2 + 1)]
                 q, j = b // NJ, b % NJ
+                acc = psum.tile([P, NBLK], F32, tag="big", bufs=NBIG, name="acc")
+                for g in range(KP):
+                    nc.tensor.matmul_mx(
+                        out=acc[:],
+                        lhsT=h0c[:, g, 2 * P * t : 2 * P * (t + 1)].bitcast(FP4X4),
+                        lhsT_scale=h0s[:, g, P * t : P * (t + 1)],
+                        rhs=cod[:, g, :].bitcast(FP4X4),
+                        rhs_scale=pl[:, g, :],
+                        start=(g == 0),
+                        stop=(g == KP - 1),
+                    )
+                nc.vector.bn_stats(out=bnr[:, t, b, :], in_=acc[:])
+                if q % 2 == 1:
+                    nc.vector.tensor_tensor(out=fo[:, t, j, q // 2, :], in0=acc[:], in1=whb, op=ALU.mult)
+                else:
+                    stg = one.tile([P, NBLK], F32, tag="stg", bufs=3, name="stg")
+                    nc.vector.tensor_tensor(out=stg[:], in0=acc[:], in1=whb, op=ALU.mult)
+                    nc.gpsimd.dma_start(out=out_block(out_0 if q == 0 else out_1, t, j), in_=stg[:])
+
+            for b in range(NB - NLAST):
+                load_w(b)
+                if b % 4 == 0 and 4 <= b <= NB - 8:
+                    for c in (NHEAD + (b - 4) // 2, NHEAD + (b - 4) // 2 + 1):
+                        spread_wh(c, "misc", 2, True)
                 for t in range(NT):
-                    acc = psum.tile([P, NBLK], F32, tag="big", bufs=NBIG, name="acc")
-                    for g in range(KP):
-                        nc.tensor.matmul_mx(
-                            out=acc[:],
-                            lhsT=h0c[:, g, 2 * P * t : 2 * P * (t + 1)].bitcast(FP4X4),
-                            lhsT_scale=h0s[:, g, P * t : P * (t + 1)],
-                            rhs=cod[:, g, :].bitcast(FP4X4),
-                            rhs_scale=pl[:, g, :],
-                            start=(g == 0),
-                            stop=(g == KP - 1),
-                        )
-                    nc.vector.bn_stats(out=bnr[:, t, b, :], in_=acc[:])
-                    if q % 2 == 1:
-                        nc.vector.tensor_tensor(out=fo[:, t, j, q // 2, :], in0=acc[:], in1=whb[:], op=ALU.mult)
-                    else:
-                        stg = one.tile([P, NBLK], F32, tag="stg", bufs=3, name="stg")
-                        nc.vector.tensor_tensor(out=stg[:], in0=acc[:], in1=whb[:], op=ALU.mult)
-                        nc.gpsimd.dma_start(out=out_block(out_0 if q == 0 else out_1, t, j), in_=stg[:])
-                    if b == NB - 1:
-                        coef(t)
+                    group(b, t)
                 if b < NB // 2:
                     make_w2(2 * b)
                     make_w2(2 * b + 1)
                 if b == NB // 2:
                     a_stats()
+            for b in range(NB - NLAST, NB):
+                load_w(b)
+            for t in range(NT):
+                for b in range(NB - NLAST, NB):
+                    group(b, t)
+                coef(t)
 
         with tc.tile_pool(name="tail", bufs=1) as tail:
             wc = tail.tile([P, H], BF16, name="wc")

@@ -59,7 +59,7 @@ def tile_multilstm_pa_kernel(
         w3f = keep.tile([P, NF32, NBLK], F32, name="w3f")
         xt_b = keep.tile([P, NT, V], BF16, name="xt_b")
         xt_f = keep.tile([P, NT, V], F32, name="xt_f")
-        fo = keep.tile([P, NT, NJ, 2, NBLK], F32, name="fo")
+        fo = keep.tile([P, NJ, 2, NT, NBLK], F32, name="fo")
         bnr = keep.tile([P, NT, NB, 6], F32, name="bnr")
         cmat = keep.tile([P, NT, 16], BF16, name="cmat")
         mask = keep.tile([P, NJ], F32, name="mask")
@@ -144,7 +144,7 @@ def tile_multilstm_pa_kernel(
             def wh_pair(c):
                 if c == NB // 2 - 1:
                     return wh_last[:]
-                return fo[:, c // NJ, c % NJ, 1, :].bitcast(BF16)
+                return fo[:, c % NJ, 1, c // NJ, :].bitcast(BF16)
 
             def spread_wh(c, tag, bufs, by_scalar):
                 wp = psum.tile([P, 2 * NBLK], BF16, tag=tag, bufs=bufs, name="wp")
@@ -282,7 +282,7 @@ def tile_multilstm_pa_kernel(
                     )
                 nc.vector.bn_stats(out=bnr[:, t, b, :], in_=acc[:])
                 if q % 2 == 1:
-                    nc.vector.tensor_tensor(out=fo[:, t, j, q // 2, :], in0=acc[:], in1=whb, op=ALU.mult)
+                    nc.vector.tensor_tensor(out=fo[:, j, q // 2, t, :], in0=acc[:], in1=whb, op=ALU.mult)
                 else:
                     stg = one.tile([P, NBLK], F32, tag="stg", bufs=3, name="stg")
                     nc.vector.tensor_tensor(out=stg[:], in0=acc[:], in1=whb, op=ALU.mult)
@@ -308,11 +308,8 @@ def tile_multilstm_pa_kernel(
                 coef(t)
 
         with tc.tile_pool(name="tail", bufs=1) as tail:
-            wc = tail.tile([P, H], BF16, name="wc")
-            bc = tail.tile([P, H], BF16, name="bc")
 
             live = {}
-            pending = []
 
             units = [(t, j) for j in range(NJ) for t in range(NT)]
 
@@ -347,7 +344,7 @@ def tile_multilstm_pa_kernel(
 
             def gates(t, j):
                 ri, rg, c0b = live[(t, j)]
-                for q, chunk in ((0, ri[:]), (2, rg[:]), (1, fo[:, t, j, 0, :]), (3, fo[:, t, j, 1, :])):
+                for q, chunk in ((0, ri[:]), (2, rg[:]), (1, fo[:, j, 0, t, :]), (3, fo[:, j, 1, t, :])):
                     pg = psum.tile([P, NBLK], F32, tag="big", bufs=NBIG, name="pg")
                     b = NJ * q + j
                     if b < NF32:
@@ -365,7 +362,7 @@ def tile_multilstm_pa_kernel(
 
             def combine(t, j):
                 ri, rg, c0b = live[(t, j)]
-                f = fo[:, t, j, 0, :]
+                f = fo[:, j, 0, t, :]
                 nc.vector.tensor_tensor(out=ri[:], in0=ri[:], in1=rg[:], op=ALU.mult)
                 nc.vector.tensor_tensor(out=f, in0=f, in1=c0b[:], op=ALU.mult)
                 nc.vector.scalar_tensor_tensor(
@@ -392,36 +389,38 @@ def tile_multilstm_pa_kernel(
                 nc.gpsimd.tensor_single_scalar(out=ve_c[:, t, :], in_=mvc[:, t, 1:2], scalar=EPS, op=ALU.add)
                 nc.gpsimd.tensor_tensor(out=rstd_c[:, t, :], in0=ve_c[:, t, :], in1=mhalf[:, t, :], op=ALU.pow)
 
-            def store_hy(queue):
-                for t, j in pending:
-                    queue.dma_start(out=out_block(out_0, t, j), in_=fo[:, t, j, 1, :])
-                pending.clear()
+            def spread(j):
+                sp = psum.tile([P, 2, NBLK], BF16, tag="big", bufs=NBIG, name="sp")
+                for h in range(2):
+                    for s in range(4):
+                        c = h * (H // P) + 4 * j + s
+                        nc.tensor.transpose(
+                            sp[:, h, P * s : P * (s + 1)], cb_col[:, c : c + 1].to_broadcast([P, P]), ident_b[:],
+                        )
+                return sp
 
-            def finish(t, j):
-                f, o = fo[:, t, j, 0, :], fo[:, t, j, 1, :]
-                cols = slice(NBLK * j, NBLK * (j + 1))
-                nc.vector.scalar_tensor_tensor(
-                    out=f, in0=f, scalar=mvc[:, t, 0:1], in1=wc[:, cols], op0=ALU.subtract, op1=ALU.mult,
+            def finish(j):
+                sp = spread(j)
+                th = tail.tile([P, NT, NBLK], F32, tag="th", bufs=2, name="th")
+                for t in range(NT):
+                    f = fo[:, j, 0, t, :]
+                    nc.vector.scalar_tensor_tensor(
+                        out=f, in0=f, scalar=mvc[:, t, 0:1], in1=sp[:, 0, :], op0=ALU.subtract, op1=ALU.mult,
+                    )
+                    nc.vector.scalar_tensor_tensor(
+                        out=f, in0=f, scalar=rstd_c[:, t, :], in1=sp[:, 1, :], op0=ALU.mult, op1=ALU.add,
+                    )
+                    nc.scalar.activation(out=th[:, t, :], in_=f, func=ACT.Tanh)
+                    nc.scalar.dma_start(out=out_block(out_1, t, j), in_=f)
+                o = fo[:, j, 1, :, :]
+                nc.gpsimd.tensor_tensor(out=o, in0=o, in1=th[:], op=ALU.mult)
+                nc.sync.dma_start(
+                    out=out_0[:, NBLK * j : NBLK * (j + 1)].rearrange("(t p) n -> p t n", p=P), in_=o,
                 )
-                nc.vector.scalar_tensor_tensor(
-                    out=f, in0=f, scalar=rstd_c[:, t, :], in1=bc[:, cols], op0=ALU.mult, op1=ALU.add,
-                )
-                th = tail.tile([P, NBLK], F32, tag="th", bufs=2, name="th")
-                nc.scalar.activation(out=th[:], in_=f, func=ACT.Tanh)
-                nc.scalar.dma_start(out=out_block(out_1, t, j), in_=f)
-                store_hy(nc.scalar)
-                nc.vector.tensor_tensor(out=o, in0=o, in1=th[:], op=ALU.mult)
-                pending.append((t, j))
 
             fetch(0)
             fetch(1)
 
-            def spread(dst, first, j):
-                sp = psum.tile([P, NBLK], BF16, tag="misc", bufs=2, name="sp")
-                for s in range(4):
-                    c = first + 4 * j + s
-                    nc.tensor.transpose(sp[:, P * s : P * (s + 1)], cb_col[:, c : c + 1].to_broadcast([P, P]), ident_b[:])
-                nc.scalar.copy(out=dst[:, NBLK * j : NBLK * (j + 1)], in_=sp[:])
 
             for q in range(4):
                 turn(NJ * q, q % 2 == 0)
@@ -434,17 +433,10 @@ def tile_multilstm_pa_kernel(
                     if u + 2 < len(units):
                         fetch(u + 2)
                     gates(t, j)
-                    if u >= NJ:
-                        if u % 2 == 0:
-                            spread(wc, 0, (u - NJ) // 2)
-                        else:
-                            spread(bc, H // P, (u - NJ) // 2)
                 if u > 0:
                     t, j = units[u - 1]
                     combine(t, j)
                     if j == NJ - 1:
                         c_stats(t)
-            for t in range(NT):
-                for j in range(NJ):
-                    finish(t, j)
-            store_hy(nc.sync)
+            for j in range(NJ):
+                finish(j)

@@ -29,6 +29,7 @@ NBIG = 5
 NF32 = 2
 WPAD = 144
 GN = 132
+NVH = 2
 NLAST = 2
 NHEAD = 4
 
@@ -412,6 +413,12 @@ def tile_multilstm_pa_kernel(
                     )
                     nc.scalar.activation(out=th[:, t, :], in_=f, func=ACT.Tanh)
                     nc.scalar.dma_start(out=out_block(out_1, t, j), in_=f)
+                if j >= NJ - NVH:
+                    for t in range(NT):
+                        o = fo[:, j, 1, t, :]
+                        nc.vector.tensor_tensor(out=o, in0=o, in1=th[:, t, :], op=ALU.mult)
+                        nc.sync.dma_start(out=out_block(out_0, t, j), in_=o)
+                    return
                 o = fo[:, j, 1, :, :]
                 nc.gpsimd.tensor_tensor(out=o, in0=o, in1=th[:], op=ALU.mult)
                 nc.sync.dma_start(

@@ -56,7 +56,7 @@ def tile_multilstm_pa_kernel(
         ident_f = keep.tile([P, P], F32, name="ident_f")
         make_identity(nc, ident_f[:])
 
-        w2t = keep.tile([P, NB - NF32, 2, NBLK], BF16, name="w2t")
+        w2t = keep.tile([P, NB - NF32, NBLK, 2], BF16, name="w2t")
         w3f = keep.tile([P, NF32, NBLK], F32, name="w3f")
         xt_b = keep.tile([P, NT, V], BF16, name="xt_b")
         xt_f = keep.tile([P, NT, V], F32, name="xt_f")
@@ -140,18 +140,19 @@ def tile_multilstm_pa_kernel(
             nc.tensor.transpose(wh_ps[:], wh_nat[:], ident_b[:])
             nc.vector.tensor_copy(out=wh_col[:], in_=wh_ps[:])
 
-            wh_last = one.tile([P, 2 * NBLK], BF16, name="wh_last")
+            wh_last = one.tile([P, NBLK], F32, name="wh_last")
+            wh_words = wh_col[:].bitcast(F32)
 
             def wh_pair(c):
                 if c == NB // 2 - 1:
                     return wh_last[:]
-                return fo[:, c % NJ, 1, c // NJ, :].bitcast(BF16)
+                return fo[:, c % NJ, 1, c // NJ, :]
 
             def spread_wh(c, tag, bufs, by_scalar):
-                wp = psum.tile([P, 2 * NBLK], BF16, tag=tag, bufs=bufs, name="wp")
-                for s in range(8):
+                wp = psum.tile([P, NBLK], F32, tag=tag, bufs=bufs, name="wp")
+                for s in range(4):
                     nc.tensor.transpose(
-                        wp[:, P * s : P * (s + 1)], wh_col[:, 8 * c + s : 8 * c + s + 1].to_broadcast([P, P]), ident_b[:],
+                        wp[:, P * s : P * (s + 1)], wh_words[:, 4 * c + s : 4 * c + s + 1].to_broadcast([P, P]), ident_f[:],
                     )
                 if by_scalar:
                     nc.scalar.copy(out=wh_pair(c), in_=wp[:])
@@ -215,11 +216,11 @@ def tile_multilstm_pa_kernel(
                         nc.scalar.activation(out=w3f[:, b, cols], in_=wn[:, s, 0:V], func=ACT.Copy, scale=wi_s)
                     else:
                         nc.scalar.activation(
-                            out=w2t[:, b - NF32, 0, cols], in_=wn[:, s, 0:V], func=ACT.Copy, scale=wi_s,
+                            out=w2t[:, b - NF32, cols, 1], in_=wn[:, s, 0:V], func=ACT.Copy, scale=wi_s,
                         )
                         nc.vector.scalar_tensor_tensor(
-                            out=w2t[:, b - NF32, 1, cols], in0=wn[:, s, 0:V], scalar=wi_s,
-                            in1=w2t[:, b - NF32, 0, cols], op0=ALU.mult, op1=ALU.subtract,
+                            out=w2t[:, b - NF32, cols, 0], in0=wn[:, s, 0:V], scalar=wi_s,
+                            in1=w2t[:, b - NF32, cols, 1], op0=ALU.mult, op1=ALU.subtract,
                         )
 
             def a_stats():
@@ -268,7 +269,11 @@ def tile_multilstm_pa_kernel(
 
             def group(b, t):
                 cod, pl = wcod[b % NBUF], wpl[b % NBUF]
-                whb = wh_pair(b // 2)[:, NBLK * (b % 2) : NBLK * (b % 2 + 1)]
+                half = NBLK // 2
+                whb = (
+                    wh_pair(b // 2)[:, half * (b % 2) : half * (b % 2 + 1)].bitcast(BF16)
+                    .rearrange("m (s p e) -> m s e p", s=2, e=2)
+                )
                 q, j = b // NJ, b % NJ
                 acc = psum.tile([P, NBLK], F32, tag="big", bufs=NBIG, name="acc")
                 for g in range(KP):
@@ -283,10 +288,16 @@ def tile_multilstm_pa_kernel(
                     )
                 nc.vector.bn_stats(out=bnr[:, t, b, :], in_=acc[:])
                 if q % 2 == 1:
-                    nc.vector.tensor_tensor(out=fo[:, j, q // 2, t, :], in0=acc[:], in1=whb, op=ALU.mult)
+                    nc.vector.tensor_tensor(
+                        out=fo[:, j, q // 2, t, :].rearrange("m (s e p) -> m s e p", s=2, e=2),
+                        in0=acc[:].rearrange("m (s e p) -> m s e p", s=2, e=2), in1=whb, op=ALU.mult,
+                    )
                 else:
                     stg = one.tile([P, NBLK], F32, tag="stg", bufs=3, name="stg")
-                    nc.vector.tensor_tensor(out=stg[:], in0=acc[:], in1=whb, op=ALU.mult)
+                    nc.vector.tensor_tensor(
+                        out=stg[:].rearrange("m (s e p) -> m s e p", s=2, e=2),
+                        in0=acc[:].rearrange("m (s e p) -> m s e p", s=2, e=2), in1=whb, op=ALU.mult,
+                    )
                     nc.gpsimd.dma_start(out=out_block(out_0 if q == 0 else out_1, t, j), in_=stg[:])
 
             for b in range(NB - NLAST):
@@ -331,13 +342,11 @@ def tile_multilstm_pa_kernel(
                         nc.tensor.transpose(tp[:, V * s : V * (s + 1)], w3f[:, b, V * s : V * (s + 1)], ident_f[:])
                     dst = w3f[:, b, :]
                 else:
-                    tp = psum.tile([P, 2, NBLK], BF16, tag="big", bufs=NBIG, name="tp")
-                    for h in range(2):
-                        for s in range(4):
-                            nc.tensor.transpose(
-                                tp[:, h, V * s : V * (s + 1)], w2t[:, b - NF32, h, V * s : V * (s + 1)], ident_b[:],
-                            )
-                    dst = w2t[:, b - NF32, :, :]
+                    tp = psum.tile([P, NBLK], F32, tag="big", bufs=NBIG, name="tp")
+                    words = w2t[:, b - NF32, :, :].rearrange("p n h -> p (n h)").bitcast(F32)
+                    for s in range(4):
+                        nc.tensor.transpose(tp[:, V * s : V * (s + 1)], words[:, V * s : V * (s + 1)], ident_f[:])
+                    dst = words
                 if by_scalar:
                     nc.scalar.copy(out=dst, in_=tp[:])
                 else:
@@ -351,8 +360,8 @@ def tile_multilstm_pa_kernel(
                     if b < NF32:
                         nc.tensor.matmul(out=pg[:], lhsT=xt_f[:, t, :], rhs=w3f[:, b, :], start=True, stop=False)
                     else:
-                        nc.tensor.matmul(out=pg[:], lhsT=xt_b[:, t, :], rhs=w2t[:, b - NF32, 0, :], start=True, stop=False)
-                        nc.tensor.matmul(out=pg[:], lhsT=xt_b[:, t, :], rhs=w2t[:, b - NF32, 1, :], start=False, stop=False)
+                        nc.tensor.matmul(out=pg[:], lhsT=xt_b[:, t, :], rhs=w2t[:, b - NF32, :, 1], start=True, stop=False)
+                        nc.tensor.matmul(out=pg[:], lhsT=xt_b[:, t, :], rhs=w2t[:, b - NF32, :, 0], start=False, stop=False)
                     nc.tensor.matmul(out=pg[:], lhsT=coeft[:, t, j, :], rhs=rows[:, q, :], start=False, stop=True)
                     nc.vector.scalar_tensor_tensor(
                         out=chunk, in0=chunk, scalar=rho[:, t, :], in1=pg[:], op0=ALU.mult, op1=ALU.add,

@@ -257,11 +257,18 @@ def tile_multilstm_pa_kernel(
             def load_w(b):
                 cod, pl = wcod[b % NBUF], wpl[b % NBUF]
                 for q4 in range(4):
-                    nc.sync.dma_start(
-                        out=pl[32 * q4 : 32 * q4 + 4, :, :].bitcast(I32),
-                        in_=w_hh1_scales[:, 4 * q4 : 4 * q4 + 4, NBLK * b : NBLK * (b + 1)]
-                        .rearrange("g r n -> r g n").bitcast(I32),
-                    )
+                    if b == 0:
+                        nc.sync.dma_start(
+                            out=pl[32 * q4 : 32 * q4 + 4, :, :].bitcast(I32),
+                            in_=w_hh1_scales[:, 4 * q4 : 4 * q4 + 4, NBLK * b : NBLK * (b + 1)]
+                            .rearrange("g r n -> r g n").bitcast(I32),
+                        )
+                    else:
+                        nc.sync.dma_start(
+                            out=pl[q4 : P : 32, :, :].bitcast(I32),
+                            in_=w_hh1_scales[:, q4 : 16 : 4, NBLK * b : NBLK * (b + 1)]
+                            .rearrange("g r n -> r g n").bitcast(I32),
+                        )
                 nc.sync.dma_start(
                     out=cod[:],
                     in_=w_hh1_words[:, :, 2 * NBLK * b : 2 * NBLK * (b + 1)].rearrange("g p n -> p g n"),

@@ -27,7 +27,7 @@ NBUF = 3
 NWN = 3
 NBIG = 5
 NF32 = 2
-WPAD = 144
+WPAD = 136
 GN = 132
 NVH = 2
 NLAST = 2
@@ -115,10 +115,10 @@ def tile_multilstm_pa_kernel(
             )
 
         with tc.tile_pool(name="stream", bufs=1) as one:
-            h0c = one.tile([P, KP, 2 * B], U8, name="h0c", align_bytes=64)
-            h0s = one.tile([P, KP, B], U8, name="h0s", align_bytes=64)
-            wcod = [one.tile([P, KP, 2 * NBLK], U8, name="wcod%d" % i, align_bytes=64) for i in range(NBUF)]
-            wpl = [one.tile([P, KP, NBLK], U8, name="wpl%d" % i, align_bytes=64) for i in range(NBUF)]
+            h0c = one.tile([P, KP, 2 * B], U8, name="h0c", align_bytes=256)
+            h0s = one.tile([P, KP, B], U8, name="h0s", align_bytes=256)
+            wcod = [one.tile([P, KP, 2 * NBLK], U8, name="wcod%d" % i, align_bytes=256) for i in range(NBUF)]
+            wpl = [one.tile([P, KP, NBLK], U8, name="wpl%d" % i, align_bytes=256) for i in range(NBUF)]
             wnat = [one.tile([P, 4, WPAD], BF16, name="wnat%d" % i) for i in range(NWN)]
 
             nc.sync.dma_start(out=h0c[:], in_=h0_words.rearrange("g p n -> p g n"))

@@ -359,9 +359,13 @@ def tile_multilstm_pa_kernel(
                 else:
                     nc.vector.tensor_copy(out=dst, in_=tp[:])
 
-            def gates(t, j):
-                ri, rg, c0b = live[(t, j)]
-                for q, chunk in ((0, ri[:]), (2, rg[:]), (1, fo[:, j, 0, t, :]), (3, fo[:, j, 1, t, :])):
+            def gates(t, j, late):
+                if late:
+                    todo = ((3, fo[:, j, 1, t, :]),)
+                else:
+                    ri, rg, c0b = live[(t, j)]
+                    todo = ((0, ri[:]), (2, rg[:]), (1, fo[:, j, 0, t, :]))
+                for q, chunk in todo:
                     pg = psum.tile([P, NBLK], F32, tag="big", bufs=NBIG, name="pg")
                     b = NJ * q + j
                     if b < NF32:
@@ -445,21 +449,27 @@ def tile_multilstm_pa_kernel(
             fetch(1)
 
 
-            for q in range(4):
-                turn(NJ * q, q % 2 == 0)
+            for q in range(3):
+                turn(NJ * q, True)
             for u in range(len(units) + 1):
                 if u < len(units):
                     t, j = units[u]
                     if t == 0 and j + 1 < NJ:
-                        for q in range(4):
-                            turn(NJ * q + j + 1, q % 2 == 0)
+                        for q in range(3):
+                            turn(NJ * q + j + 1, True)
+                    if t == 0 and j == NJ - 1:
+                        turn(NJ * 3, True)
                     if u + 2 < len(units):
                         fetch(u + 2)
-                    gates(t, j)
+                    gates(t, j, False)
                 if u > 0:
                     t, j = units[u - 1]
                     combine(t, j)
                     if j == NJ - 1:
                         c_stats(t)
             for j in range(NJ):
+                if j + 1 < NJ:
+                    turn(NJ * 3 + j + 1, True)
+                for t in range(NT):
+                    gates(t, j, True)
                 finish(j)

@@ -329,18 +329,24 @@ def tile_multilstm_pa_kernel(
         with tc.tile_pool(name="tail", bufs=1) as tail:
 
             live = {}
+            junk = tail.tile([P, NBLK], F32, name="junk")
 
-            units = [(t, j) for j in range(NJ) for t in range(NT)]
+            def by_tile(dram, j):
+                return dram[:, NBLK * j : NBLK * (j + 1)].rearrange("(t p) n -> p t n", p=P)
 
-            def fetch(u):
-                t, j = units[u]
-                ri = tail.tile([P, NBLK], F32, tag="rb", bufs=8, name="ri")
-                nc.sync.dma_start(out=ri[:], in_=out_block(out_0, t, j))
-                rg = tail.tile([P, NBLK], F32, tag="rb", bufs=8, name="rg")
-                nc.sync.dma_start(out=rg[:], in_=out_block(out_1, t, j))
-                c0b = tail.tile([P, NBLK], BF16, tag="c0b", bufs=4, name="c0b")
-                nc.sync.dma_start(out=c0b[:], in_=out_block(c0, t, j))
-                live[(t, j)] = (ri, rg, c0b)
+            def fetch(j):
+                ri = tail.tile([P, NT, NBLK], F32, tag="rb", bufs=6, name="ri")
+                rg = tail.tile([P, NT, NBLK], F32, tag="rb", bufs=6, name="rg")
+                for t in range(NT):
+                    nc.sync.dma_start(out=ri[:, t, :], in_=out_block(out_0, t, j))
+                    nc.sync.dma_start(out=rg[:, t, :], in_=out_block(out_1, t, j))
+                cp = tail.tile([P, NT, NBLK], F32, tag="cp", bufs=3, name="cp")
+                c0v = (
+                    cp[:].rearrange("p t n -> p (t n)")[:, 0 : NT * NBLK // 2].bitcast(BF16)
+                    .rearrange("p (t n) -> p t n", t=NT)
+                )
+                nc.sync.dma_start(out=c0v, in_=by_tile(c0, j))
+                live[j] = (ri, rg, cp, c0v)
 
             def turn(b, by_scalar):
                 if b < NF32:
@@ -359,13 +365,12 @@ def tile_multilstm_pa_kernel(
                 else:
                     nc.vector.tensor_copy(out=dst, in_=tp[:])
 
-            def gates(t, j, late):
-                if late:
-                    todo = ((3, fo[:, j, 1, t, :]),)
-                else:
-                    ri, rg, c0b = live[(t, j)]
-                    todo = ((0, ri[:]), (2, rg[:]), (1, fo[:, j, 0, t, :]))
-                for q, chunk in todo:
+            def gates(t, j, which):
+                for q in which:
+                    if q % 2 == 1:
+                        chunk = fo[:, j, q // 2, t, :]
+                    else:
+                        chunk = live[j][q // 2][:, t, :]
                     pg = psum.tile([P, NBLK], F32, tag="big", bufs=NBIG, name="pg")
                     b = NJ * q + j
                     if b < NF32:
@@ -381,21 +386,27 @@ def tile_multilstm_pa_kernel(
                         out=chunk, in_=chunk, func=(ACT.Tanh if q == 2 else ACT.Sigmoid), scale=rstd_a[:, t, :],
                     )
 
-            def combine(t, j):
-                ri, rg, c0b = live[(t, j)]
-                f = fo[:, j, 0, t, :]
-                nc.vector.tensor_tensor(out=ri[:], in0=ri[:], in1=rg[:], op=ALU.mult)
-                nc.vector.tensor_tensor(out=f, in0=f, in1=c0b[:], op=ALU.mult)
-                nc.vector.scalar_tensor_tensor(
-                    out=f, in0=f, scalar=1.0, in1=ri[:], op0=ALU.mult, op1=ALU.add, accum_out=csum[:, t, j : j + 1],
-                )
-                if j == 0:
-                    nc.vector.tensor_single_scalar(
-                        out=nshift[:, t, :], in_=csum[:, t, 0:1], scalar=-1.0 / NBLK, op=ALU.mult,
+            def products(j):
+                ri, rg, cp, c0v = live[j]
+                f = fo[:, j, 0, :, :]
+                nc.vector.tensor_tensor(out=f, in0=f, in1=c0v, op=ALU.mult)
+                nc.gpsimd.tensor_tensor(out=cp[:], in0=ri[:], in1=rg[:], op=ALU.mult)
+
+            def sums(j):
+                ri, rg, cp, c0v = live[j]
+                for t in range(NT):
+                    f = fo[:, j, 0, t, :]
+                    nc.vector.scalar_tensor_tensor(
+                        out=f, in0=f, scalar=1.0, in1=cp[:, t, :], op0=ALU.mult, op1=ALU.add,
+                        accum_out=csum[:, t, j : j + 1],
                     )
-                nc.scalar.activation(
-                    out=rg[:], in_=f, func=ACT.Square, bias=nshift[:, t, :], accum_out=csq[:, t, j : j + 1],
-                )
+                    if j == 0:
+                        nc.vector.tensor_single_scalar(
+                            out=nshift[:, t, :], in_=csum[:, t, 0:1], scalar=-1.0 / NBLK, op=ALU.mult,
+                        )
+                    nc.scalar.activation(
+                        out=junk[:], in_=f, func=ACT.Square, bias=nshift[:, t, :], accum_out=csq[:, t, j : j + 1],
+                    )
 
             def c_stats(t):
                 nc.vector.tensor_reduce(out=cst[:, t, 0:1], in_=csum[:, t, :], axis=AX.X, op=ALU.add)
@@ -411,7 +422,7 @@ def tile_multilstm_pa_kernel(
                 nc.gpsimd.tensor_tensor(out=rstd_c[:, t, :], in0=ve_c[:, t, :], in1=mhalf[:, t, :], op=ALU.pow)
 
             def spread(j):
-                sp = psum.tile([P, 2, NBLK], BF16, tag="big", bufs=NBIG, name="sp")
+                sp = psum.tile([P, 2, NBLK], BF16, tag="misc", bufs=2, name="sp")
                 for h in range(2):
                     for s in range(4):
                         c = h * (H // P) + 4 * j + s
@@ -422,7 +433,7 @@ def tile_multilstm_pa_kernel(
 
             def finish(j):
                 sp = spread(j)
-                th = tail.tile([P, NT, NBLK], F32, tag="th", bufs=2, name="th")
+                th = tail.tile([P, NT, NBLK], F32, tag="cp", bufs=3, name="th")
                 for t in range(NT):
                     f = fo[:, j, 0, t, :]
                     nc.vector.scalar_tensor_tensor(
@@ -448,28 +459,32 @@ def tile_multilstm_pa_kernel(
             fetch(0)
             fetch(1)
 
-
             for q in range(3):
                 turn(NJ * q, True)
-            for u in range(len(units) + 1):
-                if u < len(units):
-                    t, j = units[u]
-                    if t == 0 and j + 1 < NJ:
-                        for q in range(3):
-                            turn(NJ * q + j + 1, True)
-                    if t == 0 and j == NJ - 1:
-                        turn(NJ * 3, True)
-                    if u + 2 < len(units):
-                        fetch(u + 2)
-                    gates(t, j, False)
-                if u > 0:
-                    t, j = units[u - 1]
-                    combine(t, j)
-                    if j == NJ - 1:
-                        c_stats(t)
+            with tc.manual_schedule(engines={mybir.EngineType.DVE}):
+                for j in range(NJ):
+                    if j == 0:
+                        for t in range(NT):
+                            gates(t, j, (1,))
+                    for t in range(NT):
+                        if j + 1 < NJ:
+                            turn(NJ * (0, 2, 1)[t] + j + 1, True)
+                        elif t == 0:
+                            turn(NJ * 3, True)
+                        gates(t, j, (0, 2))
+                    if j > 0:
+                        for t in range(NT):
+                            gates(t, j, (1,))
+                        sums(j - 1)
+                    if j + 2 < NJ:
+                        fetch(j + 2)
+                    products(j)
+            sums(NJ - 1)
+            for t in range(NT):
+                c_stats(t)
             for j in range(NJ):
                 if j + 1 < NJ:
                     turn(NJ * 3 + j + 1, True)
                 for t in range(NT):
-                    gates(t, j, True)
+                    gates(t, j, (3,))
                 finish(j)

@@ -27,6 +27,7 @@ NBUF = 3
 NWN = 3
 NBIG = 5
 NF32 = 2
+F0 = 4 * (H // 512) - NF32
 WPAD = 136
 GN = 132
 NVH = 2
@@ -113,6 +114,19 @@ def tile_multilstm_pa_kernel(
                 out=coeft[:, t, :, :], in0=pc[:].unsqueeze(1).to_broadcast([P, NJ, P]),
                 in1=mask[:].unsqueeze(2).to_broadcast([P, NJ, P]), op=ALU.mult,
             )
+
+        def w2i(b):
+            return b if b < F0 else b - NF32
+
+        def turn(b, tag, bufs):
+            tp = psum.tile([P, NBLK], F32, tag=tag, bufs=bufs, name="tp")
+            if F0 <= b < F0 + NF32:
+                words = w3f[:, b - F0, :]
+            else:
+                words = w2t[:, w2i(b), :, :].rearrange("p n h -> p (n h)").bitcast(F32)
+            for s in range(4):
+                nc.tensor.transpose(tp[:, V * s : V * (s + 1)], words[:, V * s : V * (s + 1)], ident_f[:])
+            nc.scalar.copy(out=words, in_=tp[:])
 
         with tc.tile_pool(name="stream", bufs=1) as one:
             h0c = one.tile([P, KP, 2 * B], U8, name="h0c", align_bytes=256)
@@ -212,15 +226,15 @@ def tile_multilstm_pa_kernel(
                         out=gram[:], lhsT=wn[:, s, 0:V], rhs=wn[:, s, 0:GN],
                         start=(b == 0 and s == 0), stop=(b == NB - 1 and s == 3),
                     )
-                    if b < NF32:
-                        nc.scalar.activation(out=w3f[:, b, cols], in_=wn[:, s, 0:V], func=ACT.Copy, scale=wi_s)
+                    if F0 <= b < F0 + NF32:
+                        nc.scalar.activation(out=w3f[:, b - F0, cols], in_=wn[:, s, 0:V], func=ACT.Copy, scale=wi_s)
                     else:
                         nc.scalar.activation(
-                            out=w2t[:, b - NF32, cols, 1], in_=wn[:, s, 0:V], func=ACT.Copy, scale=wi_s,
+                            out=w2t[:, w2i(b), cols, 1], in_=wn[:, s, 0:V], func=ACT.Copy, scale=wi_s,
                         )
                         nc.vector.scalar_tensor_tensor(
-                            out=w2t[:, b - NF32, cols, 0], in0=wn[:, s, 0:V], scalar=wi_s,
-                            in1=w2t[:, b - NF32, cols, 1], op0=ALU.mult, op1=ALU.subtract,
+                            out=w2t[:, w2i(b), cols, 0], in0=wn[:, s, 0:V], scalar=wi_s,
+                            in1=w2t[:, w2i(b), cols, 1], op0=ALU.mult, op1=ALU.subtract,
                         )
 
             def a_stats():
@@ -325,6 +339,9 @@ def tile_multilstm_pa_kernel(
                 for b in range(NB - NLAST, NB):
                     group(b, t)
                 coef(t)
+                if t == 0:
+                    for q in (1, 0, 2):
+                        turn(NJ * q, "big", NBIG)
 
         with tc.tile_pool(name="tail", bufs=1) as tail:
 
@@ -348,23 +365,6 @@ def tile_multilstm_pa_kernel(
                 nc.sync.dma_start(out=c0v, in_=by_tile(c0, j))
                 live[j] = (ri, rg, cp, c0v)
 
-            def turn(b, by_scalar):
-                if b < NF32:
-                    tp = psum.tile([P, NBLK], F32, tag="big", bufs=NBIG, name="tf")
-                    for s in range(4):
-                        nc.tensor.transpose(tp[:, V * s : V * (s + 1)], w3f[:, b, V * s : V * (s + 1)], ident_f[:])
-                    dst = w3f[:, b, :]
-                else:
-                    tp = psum.tile([P, NBLK], F32, tag="big", bufs=NBIG, name="tp")
-                    words = w2t[:, b - NF32, :, :].rearrange("p n h -> p (n h)").bitcast(F32)
-                    for s in range(4):
-                        nc.tensor.transpose(tp[:, V * s : V * (s + 1)], words[:, V * s : V * (s + 1)], ident_f[:])
-                    dst = words
-                if by_scalar:
-                    nc.scalar.copy(out=dst, in_=tp[:])
-                else:
-                    nc.vector.tensor_copy(out=dst, in_=tp[:])
-
             def gates(t, j, which):
                 for q in which:
                     if q % 2 == 1:
@@ -373,11 +373,11 @@ def tile_multilstm_pa_kernel(
                         chunk = live[j][q // 2][:, t, :]
                     pg = psum.tile([P, NBLK], F32, tag="big", bufs=NBIG, name="pg")
                     b = NJ * q + j
-                    if b < NF32:
-                        nc.tensor.matmul(out=pg[:], lhsT=xt_f[:, t, :], rhs=w3f[:, b, :], start=True, stop=False)
+                    if F0 <= b < F0 + NF32:
+                        nc.tensor.matmul(out=pg[:], lhsT=xt_f[:, t, :], rhs=w3f[:, b - F0, :], start=True, stop=False)
                     else:
-                        nc.tensor.matmul(out=pg[:], lhsT=xt_b[:, t, :], rhs=w2t[:, b - NF32, :, 1], start=True, stop=False)
-                        nc.tensor.matmul(out=pg[:], lhsT=xt_b[:, t, :], rhs=w2t[:, b - NF32, :, 0], start=False, stop=False)
+                        nc.tensor.matmul(out=pg[:], lhsT=xt_b[:, t, :], rhs=w2t[:, w2i(b), :, 1], start=True, stop=False)
+                        nc.tensor.matmul(out=pg[:], lhsT=xt_b[:, t, :], rhs=w2t[:, w2i(b), :, 0], start=False, stop=False)
                     nc.tensor.matmul(out=pg[:], lhsT=coeft[:, t, j, :], rhs=rows[:, q, :], start=False, stop=True)
                     nc.vector.scalar_tensor_tensor(
                         out=chunk, in0=chunk, scalar=rho[:, t, :], in1=pg[:], op0=ALU.mult, op1=ALU.add,
@@ -447,7 +447,10 @@ def tile_multilstm_pa_kernel(
                 if j >= NJ - NVH:
                     for t in range(NT):
                         o = fo[:, j, 1, t, :]
-                        nc.vector.tensor_tensor(out=o, in0=o, in1=th[:, t, :], op=ALU.mult)
+                        if j == NJ - 1:
+                            nc.vector.tensor_tensor(out=o, in0=o, in1=th[:, t, :], op=ALU.mult)
+                        else:
+                            nc.gpsimd.tensor_tensor(out=o, in0=o, in1=th[:, t, :], op=ALU.mult)
                         nc.sync.dma_start(out=out_block(out_0, t, j), in_=o)
                     return
                 o = fo[:, j, 1, :, :]
@@ -459,8 +462,6 @@ def tile_multilstm_pa_kernel(
             fetch(0)
             fetch(1)
 
-            for q in range(3):
-                turn(NJ * q, True)
             with tc.manual_schedule(engines={mybir.EngineType.DVE}):
                 for j in range(NJ):
                     if j == 0:
@@ -468,9 +469,9 @@ def tile_multilstm_pa_kernel(
                             gates(t, j, (1,))
                     for t in range(NT):
                         if j + 1 < NJ:
-                            turn(NJ * (0, 2, 1)[t] + j + 1, True)
+                            turn(NJ * (0, 2, 1)[t] + j + 1, "misc", 2)
                         elif t == 0:
-                            turn(NJ * 3, True)
+                            turn(NJ * 3, "misc", 2)
                         gates(t, j, (0, 2))
                     if j > 0:
                         for t in range(NT):
@@ -484,7 +485,7 @@ def tile_multilstm_pa_kernel(
                 c_stats(t)
             for j in range(NJ):
                 if j + 1 < NJ:
-                    turn(NJ * 3 + j + 1, True)
+                    turn(NJ * 3 + j + 1, "big", NBIG)
                 for t in range(NT):
                     gates(t, j, (3,))
                 finish(j)

@@ -99,7 +99,7 @@ def tile_multilstm_pa_kernel(
 
         def coef(t):
             nc.vector.bn_aggr(out=mvr[:, t, :], in_=bnr[:, t, :, :].rearrange("p b s -> p (b s)"))
-            nc.gpsimd.tensor_single_scalar(out=ve_r[:, t, :], in_=mvr[:, t, 1:2], scalar=EPS, op=ALU.add)
+            nc.vector.tensor_single_scalar(out=ve_r[:, t, :], in_=mvr[:, t, 1:2], scalar=EPS, op=ALU.add)
             nc.gpsimd.tensor_tensor(out=rstd_r[:, t, :], in0=ve_r[:, t, :], in1=mhalf[:, t, :], op=ALU.pow)
             nc.vector.tensor_tensor(out=rho[:, t, :], in0=rstd_r[:, t, :], in1=sig_a[:, t, :], op=ALU.mult)
             nc.vector.scalar_tensor_tensor(
@@ -413,12 +413,13 @@ def tile_multilstm_pa_kernel(
                 nc.vector.tensor_reduce(out=cst[:, t, 1:2], in_=csq[:, t, :], axis=AX.X, op=ALU.add)
                 nc.vector.tensor_single_scalar(out=mvc[:, t, 0:1], in_=cst[:, t, 0:1], scalar=1.0 / H, op=ALU.mult)
                 nc.vector.tensor_tensor(out=cst[:, t, 2:3], in0=mvc[:, t, 0:1], in1=nshift[:, t, :], op=ALU.add)
-                nc.vector.tensor_tensor(out=cst[:, t, 3:4], in0=cst[:, t, 2:3], in1=cst[:, t, 2:3], op=ALU.mult)
+                nc.vector.tensor_scalar(
+                    out=cst[:, t, 3:4], in0=cst[:, t, 2:3], scalar1=cst[:, t, 2:3], scalar2=-EPS, op0=ALU.mult, op1=ALU.add,
+                )
                 nc.vector.scalar_tensor_tensor(
-                    out=mvc[:, t, 1:2], in0=cst[:, t, 1:2], scalar=1.0 / H, in1=cst[:, t, 3:4],
+                    out=ve_c[:, t, :], in0=cst[:, t, 1:2], scalar=1.0 / H, in1=cst[:, t, 3:4],
                     op0=ALU.mult, op1=ALU.subtract,
                 )
-                nc.gpsimd.tensor_single_scalar(out=ve_c[:, t, :], in_=mvc[:, t, 1:2], scalar=EPS, op=ALU.add)
                 nc.gpsimd.tensor_tensor(out=rstd_c[:, t, :], in0=ve_c[:, t, :], in1=mhalf[:, t, :], op=ALU.pow)
 
             def spread(j):
@@ -465,13 +466,15 @@ def tile_multilstm_pa_kernel(
             with tc.manual_schedule(engines={mybir.EngineType.DVE}):
                 for j in range(NJ):
                     if j == 0:
-                        for t in range(NT):
+                        for t in range(NT - 1):
                             gates(t, j, (1,))
                     for t in range(NT):
                         if j + 1 < NJ:
                             turn(NJ * (0, 2, 1)[t] + j + 1, "misc", 2)
                         elif t == 0:
                             turn(NJ * 3, "misc", 2)
+                        if j == 0 and t == NT - 1:
+                            gates(t, j, (1,))
                         gates(t, j, (0, 2))
                     if j > 0:
                         for t in range(NT):

from contextlib import ExitStack

import concourse.mybir as mybir
from concourse.masks import make_identity

F32 = mybir.dt.float32
BF16 = mybir.dt.bfloat16
U8 = mybir.dt.uint8
I32 = mybir.dt.int32
FP4X4 = mybir.dt.float4_e2m1fn_x4
ALU = mybir.AluOpType
ACT = mybir.ActivationFunctionType
AX = mybir.AxisListType

B, V, H = 384, 128, 4096
G = 4 * H
EPS = 1e-5
FLOPS = 2 * B * (H + V) * G

P = 128
NT = B // P
NBLK = 512
NB = G // NBLK
NJ = H // NBLK
KP = H // 512
NBUF = 3
NWN = 3
NBIG = 5
NF32 = 2
F0 = 4 * (H // 512) - NF32
WPAD = 136
GN = 132
NVH = 2
NLAST = 2
NHEAD = 4


def tile_multilstm_pa_kernel(
    tc, x, h0_words, h0_scales, c0, w_ih1, w_hh1_words, w_hh1_scales,
    lni_w1, lni_b1, lnh_w1, lnh_b1, lnc_w1, lnc_b1, out_0, out_1,
):
    nc = tc.nc

    def out_block(dst, t, j):
        return dst[P * t : P * (t + 1), NBLK * j : NBLK * (j + 1)]

    with ExitStack() as ctx:
        keep = ctx.enter_context(tc.tile_pool(name="keep", bufs=1))
        psum = ctx.enter_context(tc.psum_pool(name="psum", bufs=1))

        warm = keep.tile([P, 1], F32, name="warm")
        nc.vector.memset(warm[:], 0.0)
        nc.scalar.activation(out=warm[:], in_=warm[:], func=ACT.Sigmoid)

        ident_b = keep.tile([P, P], BF16, name="ident_b")
        make_identity(nc, ident_b[:])
        ident_f = keep.tile([P, P], F32, name="ident_f")
        make_identity(nc, ident_f[:])

        w2t = keep.tile([P, NB - NF32, NBLK, 2], BF16, name="w2t")
        w3f = keep.tile([P, NF32, NBLK], F32, name="w3f")
        xt_b = keep.tile([P, NT, V], BF16, name="xt_b")
        xt_f = keep.tile([P, NT, V], F32, name="xt_f")
        fo = keep.tile([P, NJ, 2, NT, NBLK], F32, name="fo")
        bnr = keep.tile([P, NT, NB, 6], F32, name="bnr")
        cmat = keep.tile([P, NT, 16], BF16, name="cmat")
        mask = keep.tile([P, NJ], F32, name="mask")
        nc.vector.tensor_reduce(
            out=mask[:], in_=ident_b[:].rearrange("p (j c) -> p j c", c=16), axis=AX.X, op=ALU.add,
        )
        coeft = keep.tile([P, NT, NJ, P], BF16, name="coeft")
        rows = keep.tile([P, 4, NBLK], BF16, name="rows")
        cb_col = keep.tile([P, P], BF16, name="cb_col")
        mhalf = keep.tile([P, NT, 1], F32, name="mhalf")
        mvr = keep.tile([P, NT, 2], F32, name="mvr")
        mvc = keep.tile([P, NT, 2], F32, name="mvc")
        ve_r = keep.tile([P, NT, 1], F32, name="ve_r")
        ve_c = keep.tile([P, NT, 1], F32, name="ve_c")
        rstd_r = keep.tile([P, NT, 1], F32, name="rstd_r")
        rstd_c = keep.tile([P, NT, 1], F32, name="rstd_c")
        rstd_a = keep.tile([P, NT, 1], F32, name="rstd_a")
        sig_a = keep.tile([P, NT, 1], F32, name="sig_a")
        rho = keep.tile([P, NT, 1], F32, name="rho")
        negc = keep.tile([P, NT, 1], F32, name="negc")
        rem_r = keep.tile([P, NT, 2], F32, name="rem_r")
        csum = keep.tile([P, NT, NJ], F32, name="csum")
        csq = keep.tile([P, NT, NJ], F32, name="csq")
        nshift = keep.tile([P, NT, 1], F32, name="nshift")
        cst = keep.tile([P, NT, 4], F32, name="cst")
        nc.vector.memset(cmat[:], 0.0)
        nc.vector.memset(mhalf[:], -0.5)

        def split3(src, rem, cm, col):
            nc.vector.tensor_copy(out=cm[:, :, col : col + 1], in_=src)
            nc.vector.tensor_tensor(out=rem[:, :, 0:1], in0=src, in1=cm[:, :, col : col + 1], op=ALU.subtract)
            nc.vector.tensor_copy(out=cm[:, :, col + 1 : col + 2], in_=rem[:, :, 0:1])
            nc.vector.tensor_tensor(out=rem[:, :, 1:2], in0=rem[:, :, 0:1], in1=cm[:, :, col + 1 : col + 2], op=ALU.subtract)
            nc.vector.tensor_copy(out=cm[:, :, col + 2 : col + 3], in_=rem[:, :, 1:2])

        def coef(t):
            nc.vector.bn_aggr(out=mvr[:, t, :], in_=bnr[:, t, :, :].rearrange("p b s -> p (b s)"))
            nc.vector.tensor_single_scalar(out=ve_r[:, t, :], in_=mvr[:, t, 1:2], scalar=EPS, op=ALU.add)
            nc.gpsimd.tensor_tensor(out=rstd_r[:, t, :], in0=ve_r[:, t, :], in1=mhalf[:, t, :], op=ALU.pow)
            nc.vector.tensor_tensor(out=rho[:, t, :], in0=rstd_r[:, t, :], in1=sig_a[:, t, :], op=ALU.mult)
            nc.vector.scalar_tensor_tensor(
                out=negc[:, t, :], in0=mvr[:, t, 0:1], scalar=-1.0, in1=rho[:, t, :], op0=ALU.mult, op1=ALU.mult,
            )
            split3(negc[:, t : t + 1, :], rem_r[:, t : t + 1, :], cmat[:, t : t + 1, :], 12)
            crep = keep.tile([P, NJ, 16], BF16, tag="crep", bufs=2, name="crep")
            nc.vector.tensor_copy(out=crep[:], in_=cmat[:, t : t + 1, :].to_broadcast([P, NJ, 16]))
            pc = psum.tile([P, P], BF16, tag="misc", bufs=2, name="pc")
            nc.tensor.transpose(pc[:], crep[:].rearrange("p j c -> p (j c)"), ident_b[:])
            nc.vector.tensor_tensor(
                out=coeft[:, t, :, :], in0=pc[:].unsqueeze(1).to_broadcast([P, NJ, P]),
                in1=mask[:].unsqueeze(2).to_broadcast([P, NJ, P]), op=ALU.mult,
            )

        def w2i(b):
            return b if b < F0 else b - NF32

        def turn(b, tag, bufs):
            tp = psum.tile([P, NBLK], F32, tag=tag, bufs=bufs, name="tp")
            if F0 <= b < F0 + NF32:
                words = w3f[:, b - F0, :]
            else:
                words = w2t[:, w2i(b), :, :].rearrange("p n h -> p (n h)").bitcast(F32)
            for s in range(4):
                nc.tensor.transpose(tp[:, V * s : V * (s + 1)], words[:, V * s : V * (s + 1)], ident_f[:])
            nc.scalar.copy(out=words, in_=tp[:])

        with tc.tile_pool(name="stream", bufs=1) as one:
            h0c = one.tile([P, KP, 2 * B], U8, name="h0c", align_bytes=256)
            h0s = one.tile([P, KP, B], U8, name="h0s", align_bytes=256)
            wcod = [one.tile([P, KP, 2 * NBLK], U8, name="wcod%d" % i, align_bytes=256) for i in range(NBUF)]
            wpl = [one.tile([P, KP, NBLK], U8, name="wpl%d" % i, align_bytes=256) for i in range(NBUF)]
            wnat = [one.tile([P, 4, WPAD], BF16, name="wnat%d" % i) for i in range(NWN)]

            nc.sync.dma_start(out=h0c[:], in_=h0_words.rearrange("g p n -> p g n"))
            nc.vector.memset(h0s[:].bitcast(I32), 0)
            for i in range(NBUF):
                nc.vector.memset(wpl[i][:].bitcast(I32), 0)
            for q4 in range(4):
                nc.sync.dma_start(
                    out=h0s[32 * q4 : 32 * q4 + 4, :, :].bitcast(I32),
                    in_=h0_scales[:, 4 * q4 : 4 * q4 + 4, :].rearrange("g r n -> r g n").bitcast(I32),
                )
            for i in range(NWN):
                nc.vector.memset(wnat[i][:], 1.0)

            wh_nat = one.tile([P, P], BF16, name="wh_nat")
            nc.scalar.dma_start(out=wh_nat[:], in_=lnh_w1.rearrange("(c p) -> c p", p=P))
            wh_col = one.tile([P, P], BF16, name="wh_col")
            wh_ps = psum.tile([P, P], BF16, tag="misc", bufs=2, name="wh_ps")
            nc.tensor.transpose(wh_ps[:], wh_nat[:], ident_b[:])
            nc.vector.tensor_copy(out=wh_col[:], in_=wh_ps[:])

            wh_last = one.tile([P, NBLK], F32, name="wh_last")
            wh_words = wh_col[:].bitcast(F32)

            def wh_pair(c):
                if c == NB // 2 - 1:
                    return wh_last[:]
                return fo[:, c % NJ, 1, c // NJ, :]

            def spread_wh(c, tag, bufs, by_scalar):
                wp = psum.tile([P, NBLK], F32, tag=tag, bufs=bufs, name="wp")
                for s in range(4):
                    nc.tensor.transpose(
                        wp[:, P * s : P * (s + 1)], wh_words[:, 4 * c + s : 4 * c + s + 1].to_broadcast([P, P]), ident_f[:],
                    )
                if by_scalar:
                    nc.scalar.copy(out=wh_pair(c), in_=wp[:])
                else:
                    nc.vector.tensor_copy(out=wh_pair(c), in_=wp[:])

            for c in range(NHEAD):
                if c < NBIG:
                    spread_wh(c, "big", NBIG, c % 2 == 0)
                else:
                    spread_wh(c, "misc", 2, c % 2 == 0)

            x_bf = one.tile([P, NT, V], BF16, name="x_bf")
            nc.scalar.dma_start(out=x_bf[:], in_=x.rearrange("(t p) k -> p t k", p=P))
            x_f = one.tile([P, NT, V], F32, name="x_f")
            nc.vector.tensor_copy(out=x_f[:], in_=x_bf[:])
            wi_nat = one.tile([P, P], BF16, name="wi_nat")
            nc.scalar.dma_start(out=wi_nat[:], in_=lni_w1.rearrange("(c p) -> c p", p=P))
            wi_col = one.tile([P, P], F32, name="wi_col")
            wi_ps = psum.tile([P, P], BF16, tag="misc", bufs=2, name="wi_ps")
            nc.tensor.transpose(wi_ps[:], wi_nat[:], ident_b[:])
            nc.vector.tensor_copy(out=wi_col[:], in_=wi_ps[:])
            cb_nat = one.tile([P, P], BF16, name="cb_nat")
            nc.vector.memset(cb_nat[:], 0.0)
            nc.scalar.dma_start(out=cb_nat[0 : H // P, :], in_=lnc_w1.rearrange("(c p) -> c p", p=P))
            nc.scalar.dma_start(out=cb_nat[H // P : 2 * H // P, :], in_=lnc_b1.rearrange("(c p) -> c p", p=P))
            cb_ps = psum.tile([P, P], BF16, tag="misc", bufs=2, name="cb_ps")
            nc.tensor.transpose(cb_ps[:], cb_nat[:], ident_b[:])
            nc.vector.tensor_copy(out=cb_col[:], in_=cb_ps[:])
            xt_ps = psum.tile([P, NT, V], F32, tag="misc", bufs=2, name="xt_ps")
            for t in range(NT):
                nc.tensor.transpose(xt_ps[:, t, :], x_f[:, t, :], ident_f[:])
            nc.vector.tensor_copy(out=xt_f[:], in_=xt_ps[:])
            xb_ps = psum.tile([P, NT, V], BF16, tag="misc", bufs=2, name="xb_ps")
            for t in range(NT):
                nc.tensor.transpose(xb_ps[:, t, :], x_bf[:, t, :], ident_b[:])
            nc.vector.tensor_copy(out=xt_b[:], in_=xb_ps[:])

            for v, vec in enumerate((lni_b1, lnh_b1, lni_w1, lnh_w1)):
                for i in range(4):
                    nc.scalar.dma_start(
                        out=rows[4 * v + i : P : 16, :, :], in_=vec.rearrange("(q j n) -> j q n", q=4, j=NJ),
                    )

            gram = psum.tile([P, GN], F32, tag="gram", bufs=1, name="gram")

            def make_w2(b):
                wn = wnat[b % NWN]
                nc.scalar.dma_start(
                    out=wn[:, :, 0:V],
                    in_=w_ih1[NBLK * b : NBLK * (b + 1), :].rearrange("(s p) k -> p s k", p=P),
                )
                for s in range(4):
                    cols = slice(V * s, V * (s + 1))
                    wi_s = wi_col[:, 4 * b + s : 4 * b + s + 1]
                    nc.tensor.matmul(
                        out=gram[:], lhsT=wn[:, s, 0:V], rhs=wn[:, s, 0:GN],
                        start=(b == 0 and s == 0), stop=(b == NB - 1 and s == 3),
                    )
                    if F0 <= b < F0 + NF32:
                        nc.scalar.activation(out=w3f[:, b - F0, cols], in_=wn[:, s, 0:V], func=ACT.Copy, scale=wi_s)
                    else:
                        nc.scalar.activation(
                            out=w2t[:, w2i(b), cols, 1], in_=wn[:, s, 0:V], func=ACT.Copy, scale=wi_s,
                        )
                        nc.vector.scalar_tensor_tensor(
                            out=w2t[:, w2i(b), cols, 0], in0=wn[:, s, 0:V], scalar=wi_s,
                            in1=w2t[:, w2i(b), cols, 1], op0=ALU.mult, op1=ALU.subtract,
                        )

            def a_stats():
                gs = one.tile([P, GN], F32, name="gs")
                nc.vector.tensor_copy(out=gs[:], in_=gram[:])
                y = psum.tile([P, NT, GN], F32, tag="misc", bufs=2, name="y")
                for t in range(NT):
                    nc.tensor.matmul(out=y[:, t, :], lhsT=xt_f[:, t, :], rhs=gs[:], start=True, stop=True)
                ssq = one.tile([P, NT, 1], F32, name="ssq")
                prod = one.tile([P, V], F32, name="prod")
                for t in range(NT):
                    nc.vector.scalar_tensor_tensor(
                        out=prod[:], in0=y[:, t, 0:V], scalar=1.0, in1=x_f[:, t, :],
                        op0=ALU.mult, op1=ALU.mult, accum_out=ssq[:, t, :],
                    )
                mean_a = one.tile([P, NT, 1], F32, name="mean_a")
                nc.vector.tensor_single_scalar(out=mean_a[:], in_=y[:, :, V : V + 1], scalar=1.0 / G, op=ALU.mult)
                msq = one.tile([P, NT, 1], F32, name="msq")
                nc.vector.tensor_tensor(out=msq[:], in0=mean_a[:], in1=mean_a[:], op=ALU.mult)
                var_a = one.tile([P, NT, 1], F32, name="var_a")
                nc.vector.scalar_tensor_tensor(
                    out=var_a[:], in0=ssq[:], scalar=1.0 / G, in1=msq[:], op0=ALU.mult, op1=ALU.subtract,
                )
                nc.gpsimd.tensor_single_scalar(out=var_a[:], in_=var_a[:], scalar=EPS, op=ALU.add)
                nc.gpsimd.tensor_tensor(out=rstd_a[:], in0=var_a[:], in1=mhalf[:], op=ALU.pow)
                nc.vector.tensor_tensor(out=sig_a[:], in0=var_a[:], in1=rstd_a[:], op=ALU.mult)
                negma = one.tile([P, NT, 1], F32, name="negma")
                nc.vector.tensor_single_scalar(out=negma[:], in_=mean_a[:], scalar=-1.0, op=ALU.mult)
                rem_a = one.tile([P, NT, 2], F32, name="rem_a")
                split3(sig_a[:], rem_a, cmat, 0)
                nc.vector.tensor_copy(out=cmat[:, :, 4:7], in_=cmat[:, :, 0:3])
                split3(negma[:], rem_a, cmat, 8)

            def load_w(b):
                cod, pl = wcod[b % NBUF], wpl[b % NBUF]
                for q4 in range(4):
                    if b == 0:
                        nc.sync.dma_start(
                            out=pl[32 * q4 : 32 * q4 + 4, :, :].bitcast(I32),
                            in_=w_hh1_scales[:, 4 * q4 : 4 * q4 + 4, NBLK * b : NBLK * (b + 1)]
                            .rearrange("g r n -> r g n").bitcast(I32),
                        )
                    else:
                        nc.sync.dma_start(
                            out=pl[q4 : P : 32, :, :].bitcast(I32),
                            in_=w_hh1_scales[:, q4 : 16 : 4, NBLK * b : NBLK * (b + 1)]
                            .rearrange("g r n -> r g n").bitcast(I32),
                        )
                nc.sync.dma_start(
                    out=cod[:],
                    in_=w_hh1_words[:, :, 2 * NBLK * b : 2 * NBLK * (b + 1)].rearrange("g p n -> p g n"),
                )

            def group(b, t):
                cod, pl = wcod[b % NBUF], wpl[b % NBUF]
                half = NBLK // 2
                whb = (
                    wh_pair(b // 2)[:, half * (b % 2) : half * (b % 2 + 1)].bitcast(BF16)
                    .rearrange("m (s p e) -> m s e p", s=2, e=2)
                )
                q, j = b // NJ, b % NJ
                acc = psum.tile([P, NBLK], F32, tag="big", bufs=NBIG, name="acc")
                for g in range(KP):
                    nc.tensor.matmul_mx(
                        out=acc[:],
                        lhsT=h0c[:, g, 2 * P * t : 2 * P * (t + 1)].bitcast(FP4X4),
                        lhsT_scale=h0s[:, g, P * t : P * (t + 1)],
                        rhs=cod[:, g, :].bitcast(FP4X4),
                        rhs_scale=pl[:, g, :],
                        start=(g == 0),
                        stop=(g == KP - 1),
                    )
                nc.vector.bn_stats(out=bnr[:, t, b, :], in_=acc[:])
                if q % 2 == 1:
                    nc.vector.tensor_tensor(
                        out=fo[:, j, q // 2, t, :].rearrange("m (s e p) -> m s e p", s=2, e=2),
                        in0=acc[:].rearrange("m (s e p) -> m s e p", s=2, e=2), in1=whb, op=ALU.mult,
                    )
                else:
                    stg = one.tile([P, NBLK], F32, tag="stg", bufs=3, name="stg")
                    nc.vector.tensor_tensor(
                        out=stg[:].rearrange("m (s e p) -> m s e p", s=2, e=2),
                        in0=acc[:].rearrange("m (s e p) -> m s e p", s=2, e=2), in1=whb, op=ALU.mult,
                    )
                    nc.gpsimd.dma_start(out=out_block(out_0 if q == 0 else out_1, t, j), in_=stg[:])

            for b in range(NB - NLAST):
                load_w(b)
                if b % 4 == 0 and 4 <= b <= NB - 8:
                    for c in (NHEAD + (b - 4) // 2, NHEAD + (b - 4) // 2 + 1):
                        spread_wh(c, "misc", 2, True)
                for t in range(NT):
                    group(b, t)
                if b < NB // 2:
                    make_w2(2 * b)
                    make_w2(2 * b + 1)
                if b == NB // 2:
                    a_stats()
            for b in range(NB - NLAST, NB):
                load_w(b)
            for t in range(NT):
                for b in range(NB - NLAST, NB):
                    group(b, t)
                coef(t)
                if t == 0:
                    for q in (1, 0, 2):
                        turn(NJ * q, "big", NBIG)

        with tc.tile_pool(name="tail", bufs=1) as tail:

            live = {}
            junk = tail.tile([P, NBLK], F32, name="junk")

            def by_tile(dram, j):
                return dram[:, NBLK * j : NBLK * (j + 1)].rearrange("(t p) n -> p t n", p=P)

            def fetch(j):
                ri = tail.tile([P, NT, NBLK], F32, tag="rb", bufs=6, name="ri")
                rg = tail.tile([P, NT, NBLK], F32, tag="rb", bufs=6, name="rg")
                for t in range(NT):
                    nc.sync.dma_start(out=ri[:, t, :], in_=out_block(out_0, t, j))
                    nc.sync.dma_start(out=rg[:, t, :], in_=out_block(out_1, t, j))
                cp = tail.tile([P, NT, NBLK], F32, tag="cp", bufs=3, name="cp")
                c0v = (
                    cp[:].rearrange("p t n -> p (t n)")[:, 0 : NT * NBLK // 2].bitcast(BF16)
                    .rearrange("p (t n) -> p t n", t=NT)
                )
                nc.sync.dma_start(out=c0v, in_=by_tile(c0, j))
                live[j] = (ri, rg, cp, c0v)

            def gates(t, j, which):
                for q in which:
                    if q % 2 == 1:
                        chunk = fo[:, j, q // 2, t, :]
                    else:
                        chunk = live[j][q // 2][:, t, :]
                    pg = psum.tile([P, NBLK], F32, tag="big", bufs=NBIG, name="pg")
                    b = NJ * q + j
                    if F0 <= b < F0 + NF32:
                        nc.tensor.matmul(out=pg[:], lhsT=xt_f[:, t, :], rhs=w3f[:, b - F0, :], start=True, stop=False)
                    else:
                        nc.tensor.matmul(out=pg[:], lhsT=xt_b[:, t, :], rhs=w2t[:, w2i(b), :, 1], start=True, stop=False)
                        nc.tensor.matmul(out=pg[:], lhsT=xt_b[:, t, :], rhs=w2t[:, w2i(b), :, 0], start=False, stop=False)
                    nc.tensor.matmul(out=pg[:], lhsT=coeft[:, t, j, :], rhs=rows[:, q, :], start=False, stop=True)
                    nc.vector.scalar_tensor_tensor(
                        out=chunk, in0=chunk, scalar=rho[:, t, :], in1=pg[:], op0=ALU.mult, op1=ALU.add,
                    )
                    nc.scalar.activation(
                        out=chunk, in_=chunk, func=(ACT.Tanh if q == 2 else ACT.Sigmoid), scale=rstd_a[:, t, :],
                    )

            def products(j):
                ri, rg, cp, c0v = live[j]
                f = fo[:, j, 0, :, :]
                nc.vector.tensor_tensor(out=f, in0=f, in1=c0v, op=ALU.mult)
                nc.gpsimd.tensor_tensor(out=cp[:], in0=ri[:], in1=rg[:], op=ALU.mult)

            def sums(j):
                ri, rg, cp, c0v = live[j]
                for t in range(NT):
                    f = fo[:, j, 0, t, :]
                    nc.vector.scalar_tensor_tensor(
                        out=f, in0=f, scalar=1.0, in1=cp[:, t, :], op0=ALU.mult, op1=ALU.add,
                        accum_out=csum[:, t, j : j + 1],
                    )
                    if j == 0:
                        nc.vector.tensor_single_scalar(
                            out=nshift[:, t, :], in_=csum[:, t, 0:1], scalar=-1.0 / NBLK, op=ALU.mult,
                        )
                    nc.scalar.activation(
                        out=junk[:], in_=f, func=ACT.Square, bias=nshift[:, t, :], accum_out=csq[:, t, j : j + 1],
                    )

            def c_stats(t):
                nc.vector.tensor_reduce(out=cst[:, t, 0:1], in_=csum[:, t, :], axis=AX.X, op=ALU.add)
                nc.vector.tensor_reduce(out=cst[:, t, 1:2], in_=csq[:, t, :], axis=AX.X, op=ALU.add)
                nc.vector.tensor_single_scalar(out=mvc[:, t, 0:1], in_=cst[:, t, 0:1], scalar=1.0 / H, op=ALU.mult)
                nc.vector.tensor_tensor(out=cst[:, t, 2:3], in0=mvc[:, t, 0:1], in1=nshift[:, t, :], op=ALU.add)
                nc.vector.tensor_scalar(
                    out=cst[:, t, 3:4], in0=cst[:, t, 2:3], scalar1=cst[:, t, 2:3], scalar2=-EPS, op0=ALU.mult, op1=ALU.add,
                )
                nc.vector.scalar_tensor_tensor(
                    out=ve_c[:, t, :], in0=cst[:, t, 1:2], scalar=1.0 / H, in1=cst[:, t, 3:4],
                    op0=ALU.mult, op1=ALU.subtract,
                )
                nc.gpsimd.tensor_tensor(out=rstd_c[:, t, :], in0=ve_c[:, t, :], in1=mhalf[:, t, :], op=ALU.pow)

            def spread(j):
                sp = psum.tile([P, 2, NBLK], BF16, tag="misc", bufs=2, name="sp")
                for h in range(2):
                    for s in range(4):
                        c = h * (H // P) + 4 * j + s
                        nc.tensor.transpose(
                            sp[:, h, P * s : P * (s + 1)], cb_col[:, c : c + 1].to_broadcast([P, P]), ident_b[:],
                        )
                return sp

            def finish(j):
                sp = spread(j)
                th = tail.tile([P, NT, NBLK], F32, tag="cp", bufs=3, name="th")
                for t in range(NT):
                    f = fo[:, j, 0, t, :]
                    nc.vector.scalar_tensor_tensor(
                        out=f, in0=f, scalar=mvc[:, t, 0:1], in1=sp[:, 0, :], op0=ALU.subtract, op1=ALU.mult,
                    )
                    nc.vector.scalar_tensor_tensor(
                        out=f, in0=f, scalar=rstd_c[:, t, :], in1=sp[:, 1, :], op0=ALU.mult, op1=ALU.add,
                    )
                    nc.scalar.activation(out=th[:, t, :], in_=f, func=ACT.Tanh)
                    nc.scalar.dma_start(out=out_block(out_1, t, j), in_=f)
                if j >= NJ - NVH:
                    for t in range(NT):
                        o = fo[:, j, 1, t, :]
                        if j == NJ - 1:
                            nc.vector.tensor_tensor(out=o, in0=o, in1=th[:, t, :], op=ALU.mult)
                        else:
                            nc.gpsimd.tensor_tensor(out=o, in0=o, in1=th[:, t, :], op=ALU.mult)
                        nc.sync.dma_start(out=out_block(out_0, t, j), in_=o)
                    return
                o = fo[:, j, 1, :, :]
                nc.gpsimd.tensor_tensor(out=o, in0=o, in1=th[:], op=ALU.mult)
                nc.sync.dma_start(
                    out=out_0[:, NBLK * j : NBLK * (j + 1)].rearrange("(t p) n -> p t n", p=P), in_=o,
                )

            fetch(0)
            fetch(1)

            with tc.manual_schedule(engines={mybir.EngineType.DVE}):
                for j in range(NJ):
                    if j == 0:
                        for t in range(NT - 1):
                            gates(t, j, (1,))
                    for t in range(NT):
                        if j + 1 < NJ:
                            turn(NJ * (0, 2, 1)[t] + j + 1, "misc", 2)
                        elif t == 0:
                            turn(NJ * 3, "misc", 2)
                        if j == 0 and t == NT - 1:
                            gates(t, j, (1,))
                        gates(t, j, (0, 2))
                    if j > 0:
                        for t in range(NT):
                            gates(t, j, (1,))
                        sums(j - 1)
                    if j + 2 < NJ:
                        fetch(j + 2)
                    products(j)
            sums(NJ - 1)
            for t in range(NT):
                c_stats(t)
            for j in range(NJ):
                if j + 1 < NJ:
                    turn(NJ * 3 + j + 1, "big", NBIG)
                for t in range(NT):
                    gates(t, j, (3,))
                finish(j)
